import numpy as np
import ml_dtypes


def mxq(x, axis, fmt="e4m3"):
    dtype, down = {"e4m3": (ml_dtypes.float8_e4m3fn, 7), "e5m2": (ml_dtypes.float8_e5m2, 14)}[fmt]
    v = np.moveaxis(np.asarray(x, np.float32).astype(ml_dtypes.bfloat16).astype(np.float64), axis, -1)
    blocks = v.reshape(v.shape[:-1] + (-1, 32))
    amax = np.abs(blocks).max(-1, keepdims=True)
    byte = np.maximum(np.where(amax > 0, np.frexp(amax)[1] - 1 + 127, 0) - down, 1)
    scale = np.exp2(byte - 127.0)
    codes = (blocks / scale).astype(np.float32).astype(dtype).astype(np.float64)
    return np.moveaxis((codes * scale).reshape(v.shape), -1, axis)


WIDE = False


def mx_kscale(k):
    if not WIDE:
        return np.ones(k)
    levels = np.array([10, -10, 5, -5, 0])
    a = np.random.permutation(np.resize(levels, k // 512 * 4)).reshape(k // 512, 4)
    idx = np.arange(k)
    return np.exp2(a[idx // 512, idx % 128 // 32])


BF16 = ml_dtypes.bfloat16


def bf(x):
    return np.asarray(x, np.float32).astype(BF16)


def f64(x):
    return np.asarray(x).astype(np.float64)


E2M1 = np.array([0.0, 0.5, 1.0, 1.5, 2.0, 3.0, 4.0, 6.0, -0.0, -0.5, -1.0, -1.5, -2.0, -3.0, -4.0, -6.0])


def pack_weight(w, fmt):
    k, n = w.shape
    w = f64(bf(w)).reshape(k // 32, 32, n)
    amax = np.abs(w).max(1)
    if fmt == "e4m3":
        byte = np.frexp(amax)[1] - 1 + 127 - 7
    else:
        mant, ex = np.frexp(amax / 6.0)
        byte = np.where(mant > 0.5, ex, ex - 1) + 127
    byte = np.clip(np.where(amax > 0, byte, 1), 1, 254)
    scaled = (w * np.exp2(127.0 - byte)[:, None, :]).reshape(k, n).astype(np.float32)
    by_word = np.ascontiguousarray(scaled.reshape(k // 512, 128, 4, n).transpose(0, 1, 3, 2))
    if fmt == "e4m3":
        words = by_word.astype(ml_dtypes.float8_e4m3fn).view(np.uint8)
    else:
        c = by_word.astype(ml_dtypes.float4_e2m1fn).view(np.uint8) & 0xF
        words = c[..., 0::2] | (c[..., 1::2] << 4)
    return np.ascontiguousarray(words), np.ascontiguousarray(byte.astype(np.uint8).reshape(k // 512, 16, n))


def unpack_weight(words, scales, fmt):
    g, p, n, _ = words.shape
    if fmt == "e4m3":
        vals = np.ascontiguousarray(words).view(ml_dtypes.float8_e4m3fn).astype(np.float64)
    else:
        nib = np.empty((g, p, n, 4), np.uint8)
        nib[..., 0::2] = words & 0xF
        nib[..., 1::2] = words >> 4
        vals = E2M1[nib]
    vals = vals * np.repeat(np.exp2(scales.astype(np.float64) - 127.0), 8, axis=1)[..., None]
    return vals.transpose(0, 1, 3, 2).reshape(g * 512, n)


B, N, D = 128, 17, 1024
LN_EPS = 1e-5
LEAKY_SLOPE = 0.01
FMT = "e4m3"


def setup_inputs():
    s = mx_kscale(D)
    s = s / s.max()
    h = bf(np.random.standard_normal((B, N, D)) * 0.5 * s)
    W_l = np.random.standard_normal((D, D)) * 2.0 / np.sqrt(D) / s[None, :]
    W_l_words, W_l_scales = pack_weight(np.ascontiguousarray(W_l.T), FMT)
    b_l = bf(np.random.standard_normal(D) * 0.1)
    W_r = np.random.standard_normal((D, D)) * 1.0 / np.sqrt(D) / s[None, :]
    W_r_words, W_r_scales = pack_weight(np.ascontiguousarray(W_r.T), FMT)
    ln_g = bf(1.0 + 0.1 * np.random.standard_normal(D))
    ln_b = bf(-0.4 + 0.2 * np.random.standard_normal(D))
    return {"h": h,
            "W_l_words": W_l_words,
            "W_l_scales": W_l_scales,
            "b_l": b_l,
            "W_r_words": W_r_words,
            "W_r_scales": W_r_scales,
            "ln_g": ln_g,
            "ln_b": ln_b}


def reference(h, W_l_words, W_l_scales, b_l, W_r_words, W_r_scales, ln_g, ln_b):
    h = f64(h)
    n = h.shape[1]
    mean_neigh = (np.sum(h, axis=1, keepdims=True) - h) / (n - 1)
    c = ((mxq(mean_neigh, 2, "e4m3") @ unpack_weight(W_l_words, W_l_scales, FMT)) + f64(b_l)
         + (mxq(h, 2, "e4m3") @ unpack_weight(W_r_words, W_r_scales, FMT)))
    mu = np.mean(c, axis=-1, keepdims=True)
    var = np.mean(np.square(c - mu), axis=-1, keepdims=True)
    y = (c - mu) * (1.0 / np.sqrt(var + LN_EPS)) * f64(ln_g) + f64(ln_b)
    a = np.where(y > 0, y, LEAKY_SLOPE * y)
    return a + h

@@ -1,0 +1,227 @@
+from contextlib import ExitStack
+
+import concourse.mybir as mybir
+from concourse.masks import make_identity
+
+F32 = mybir.dt.float32
+BF16 = mybir.dt.bfloat16
+I32 = mybir.dt.int32
+U32 = mybir.dt.uint32
+U8 = mybir.dt.uint8
+FP8X4 = mybir.dt.float8_e4m3fn_x4
+ALU = mybir.AluOpType
+ACT = mybir.ActivationFunctionType
+
+P = 128
+NODES = 17
+D = 1024
+PACK = 4
+K_PASS = P * PACK
+PASSES = D // K_PASS
+N_TILE = 512
+HALVES = D // N_TILE
+LN_EPS = 1e-5
+LEAKY_SLOPE = 0.01
+LOAD_NODES = 4
+AHEAD_PRODUCTS = 2
+AHEAD_TRANSPOSE = 3
+
+FLOPS = 2 * 2 * P * NODES * D * D
+
+
+def tile_gnnnicheencoder_pa_kernel(
+    tc, h, W_l_words, W_l_scales, b_l, W_r_words, W_r_scales, ln_g, ln_b, out
+):
+    nc = tc.nc
+    weights = ((W_r_words, W_r_scales), (W_l_words, W_l_scales))
+
+    with ExitStack() as stack:
+        keep = stack.enter_context(tc.tile_pool(name="keep", bufs=1))
+        sides = stack.enter_context(tc.tile_pool(name="sides", bufs=4))
+        work = stack.enter_context(tc.tile_pool(name="work", bufs=3))
+        small = stack.enter_context(tc.tile_pool(name="small", bufs=4))
+        psum_keep = stack.enter_context(tc.psum_pool(name="psum_keep", bufs=1))
+        banks = stack.enter_context(tc.psum_pool(name="banks", bufs=4))
+
+        h_sb = keep.tile([P, NODES, D], BF16)
+        for first in range(0, NODES, LOAD_NODES):
+            nodes = slice(first, min(first + LOAD_NODES, NODES))
+            nc.sync.dma_start(out=h_sb[:, nodes, :], in_=h[:, nodes, :])
+
+        w_planes = keep.tile([P, 2, PASSES, D], U8, align_bytes=64)
+        nc.vector.memset(w_planes[:].bitcast(I32), 0)
+        for w, (words, scales) in enumerate(weights):
+            for quad in range(4):
+                nc.sync.dma_start(
+                    out=w_planes[32 * quad : 32 * quad + 4, w, :, :].bitcast(I32),
+                    in_=scales[:, 4 * quad : 4 * quad + 4, :].rearrange("g r n -> r g n").bitcast(I32),
+                )
+        w_words = keep.tile([P, 2, PASSES, D], U32, align_bytes=64)
+        for w, (words, scales) in enumerate(weights):
+            for g in range(PASSES):
+                nc.sync.dma_start(
+                    out=w_words[:, w, g, :].bitcast(I32),
+                    in_=words[g].rearrange("p n t -> p (n t)").bitcast(I32),
+                )
+
+        ident_f32 = keep.tile([P, P], F32)
+        make_identity(nc, ident_f32[:])
+        ident_bf16 = keep.tile([P, P], BF16)
+        make_identity(nc, ident_bf16[:])
+        ones = keep.tile([P, P], BF16)
+        nc.vector.memset(ones[:], 1.0)
+        eps = keep.tile([P, 1], F32)
+        nc.vector.memset(eps[:], LN_EPS)
+
+        rows = keep.tile([P, 3, D], BF16)
+        nc.vector.memset(rows[:].bitcast(I32), 0)
+        for j, vec in enumerate((b_l, ln_g, ln_b)):
+            nc.scalar.dma_start(out=rows[0:1, j, :], in_=vec.unsqueeze(0))
+
+        total = [banks.tile([P, K_PASS], F32, tag="bank", name="total%d" % g) for g in range(PASSES)]
+        for i in range(NODES):
+            for g in range(PASSES):
+                nc.tensor.matmul(
+                    out=total[g][:],
+                    lhsT=ident_bf16[:],
+                    rhs=h_sb[:, i, g * K_PASS : (g + 1) * K_PASS],
+                    start=(i == 0),
+                    stop=(i == NODES - 1),
+                )
+
+        bias_ps = banks.tile([P, D], BF16, tag="bank")
+        gain_ps = psum_keep.tile([P, D], BF16)
+        shift_ps = psum_keep.tile([P, D], BF16)
+        for j, spread in enumerate((bias_ps, gain_ps, shift_ps)):
+            for half in range(HALVES):
+                cols = slice(half * N_TILE, (half + 1) * N_TILE)
+                nc.tensor.matmul(out=spread[:, cols], lhsT=ones[:], rhs=rows[:, j, cols], start=True, stop=True)
+        bias_sb = keep.tile([P, D], BF16)
+        nc.scalar.copy(out=bias_sb[:], in_=bias_ps[:])
+
+        h_side = {}
+        m_side = {}
+        product = {}
+
+        def transpose_and_quantise_h(i):
+            pairs = h_sb[:, i, :].bitcast(F32)
+            flipped = banks.tile([P, PASSES, 2, P], F32, tag="bank")
+            for g in range(PASSES):
+                for u in range(2):
+                    nc.tensor.transpose(
+                        out=flipped[:, g, u, :],
+                        in_=pairs[:, 256 * g + u : 256 * (g + 1) : 2],
+                        identity=ident_f32[:],
+                    )
+            h_t = sides.tile([P, D], BF16, align_bytes=64)
+            nc.scalar.copy(
+                out=h_t[:].bitcast(F32).rearrange("p (g b u) -> p g b u", g=PASSES, u=2),
+                in_=flipped[:].rearrange("p g u b -> p g b u"),
+            )
+            h_codes = sides.tile([P, PASSES * P], U32, align_bytes=64)
+            h_plane = sides.tile([P, PASSES * P], U8, align_bytes=64)
+            nc.vector.quantize_mx(out=h_codes[:].bitcast(FP8X4), scales=h_plane[:], in_=h_t[:])
+            h_side[i] = (h_t, h_codes, h_plane)
+
+        def mean_of_neighbours(i):
+            h_t = h_side[i][0]
+            m_t = sides.tile([P, D], BF16, align_bytes=64)
+            for g in range(PASSES):
+                cols = slice(g * K_PASS, (g + 1) * K_PASS)
+                nc.vector.scalar_tensor_tensor(
+                    out=m_t[:, cols].rearrange("p (b t) -> p b t", t=PACK),
+                    in0=h_t[:, cols].rearrange("p (b t) -> p b t", t=PACK),
+                    scalar=-1.0 / (NODES - 1),
+                    in1=total_t[g][:].rearrange("p t b -> p b t"),
+                    op0=ALU.mult,
+                    op1=ALU.add,
+                )
+            m_codes = sides.tile([P, PASSES * P], U32, align_bytes=64)
+            m_plane = sides.tile([P, PASSES * P], U8, align_bytes=64)
+            nc.vector.quantize_mx(out=m_codes[:].bitcast(FP8X4), scales=m_plane[:], in_=m_t[:])
+            m_side[i] = (m_codes, m_plane)
+
+        def multiply(i):
+            operands = (h_side[i][1:], m_side[i])
+            product[i] = []
+            for half in range(HALVES):
+                cols = slice(half * N_TILE, (half + 1) * N_TILE)
+                acc = banks.tile([P, N_TILE], F32, tag="bank")
+                for w, (codes, plane) in enumerate(operands):
+                    for g in range(PASSES):
+                        graphs = slice(g * P, (g + 1) * P)
+                        nc.tensor.matmul_mx(
+                            out=acc[:],
+                            lhsT=codes[:, graphs].bitcast(FP8X4),
+                            lhsT_scale=plane[:, graphs],
+                            rhs=w_words[:, w, g, cols].bitcast(FP8X4),
+                            rhs_scale=w_planes[:, w, g, cols],
+                            start=(w == 0 and g == 0),
+                            stop=(w == 1 and g == PASSES - 1),
+                        )
+                product[i].append(acc)
+
+        for i in range(AHEAD_TRANSPOSE):
+            transpose_and_quantise_h(i)
+        total_sb = keep.tile([P, PASSES, PACK, P], F32)
+        scaled_copy = (nc.scalar.mul, nc.vector.tensor_scalar_mul)
+        for g in range(PASSES):
+            scaled_copy[g](total_sb[:, g], total[g][:].rearrange("b (p t) -> b t p", t=PACK), 1.0 / (NODES - 1))
+        total_t = [psum_keep.tile([P, PACK, P], F32, name="total_t%d" % g) for g in range(PASSES)]
+        for g in range(PASSES):
+            for t in range(PACK):
+                nc.tensor.transpose(out=total_t[g][:, t, :], in_=total_sb[:, g, t, :], identity=ident_f32[:])
+
+        for i in range(AHEAD_PRODUCTS):
+            mean_of_neighbours(i)
+            multiply(i)
+
+        for i in range(NODES):
+            c = work.tile([P, D], F32)
+            sums = small.tile([P, HALVES], F32)
+            for half in range(HALVES):
+                cols = slice(half * N_TILE, (half + 1) * N_TILE)
+                nc.vector.scalar_tensor_tensor(
+                    out=c[:, cols],
+                    in0=product[i][half][:],
+                    scalar=1.0,
+                    in1=bias_sb[:, cols],
+                    op0=ALU.mult,
+                    op1=ALU.add,
+                    accum_out=sums[:, half : half + 1],
+                )
+            neg_mean = small.tile([P, 1], F32)
+            nc.vector.tensor_scalar(
+                out=neg_mean[:], in0=sums[:, 0:1], scalar1=sums[:, 1:2], scalar2=-1.0 / D, op0=ALU.add, op1=ALU.mult
+            )
+            squares = work.tile([P, D], BF16)
+            sum_sq = small.tile([P, 1], F32)
+            nc.scalar.activation(
+                out=squares[:], in_=c[:], func=ACT.Square, bias=neg_mean[:], scale=1.0, accum_out=sum_sq[:]
+            )
+            std = small.tile([P, 1], F32)
+            nc.scalar.activation(out=std[:], in_=sum_sq[:], func=ACT.Sqrt, bias=eps[:], scale=1.0 / D)
+            centred = work.tile([P, D], F32)
+            nc.vector.scalar_tensor_tensor(
+                out=centred[:], in0=c[:], scalar=neg_mean[:], in1=gain_ps[:], op0=ALU.add, op1=ALU.mult
+            )
+
+            if i + AHEAD_TRANSPOSE < NODES:
+                transpose_and_quantise_h(i + AHEAD_TRANSPOSE)
+            if i + AHEAD_PRODUCTS < NODES:
+                mean_of_neighbours(i + AHEAD_PRODUCTS)
+                multiply(i + AHEAD_PRODUCTS)
+
+            rstd = small.tile([P, 1], F32)
+            nc.vector.reciprocal(out=rstd[:], in_=std[:])
+            y = work.tile([P, D], F32)
+            nc.vector.scalar_tensor_tensor(
+                out=y[:], in0=centred[:], scalar=rstd[:], in1=shift_ps[:], op0=ALU.mult, op1=ALU.add
+            )
+            lift = work.tile([P, D], F32)
+            nc.scalar.activation(out=lift[:], in_=y[:], func=ACT.Relu, scale=-(1.0 - LEAKY_SLOPE))
+            y_plus_h = work.tile([P, D], F32)
+            nc.gpsimd.tensor_tensor(out=y_plus_h[:], in0=y[:], in1=h_sb[:, i, :], op=ALU.add)
+            result = work.tile([P, D], F32)
+            nc.gpsimd.tensor_tensor(out=result[:], in0=y_plus_h[:], in1=lift[:], op=ALU.add)
+            nc.sync.dma_start(out=out[:, i, :], in_=result[:])

@@ -43,13 +43,30 @@ def tile_gnnnicheencoder_pa_kernel(
         psum_keep = stack.enter_context(tc.psum_pool(name="psum_keep", bufs=1))
         banks = stack.enter_context(tc.psum_pool(name="banks", bufs=4))
 
-        h_sb = keep.tile([P, NODES, D], BF16)
-        for first in range(0, NODES, LOAD_NODES):
-            nodes = slice(first, min(first + LOAD_NODES, NODES))
-            nc.sync.dma_start(out=h_sb[:, nodes, :], in_=h[:, nodes, :])
-
+        rows = keep.tile([P, 3, D], BF16)
+        nc.vector.memset(rows[:].bitcast(I32), 0)
         w_planes = keep.tile([P, 2, PASSES, D], U8, align_bytes=64)
         nc.vector.memset(w_planes[:].bitcast(I32), 0)
+        ones = keep.tile([P, P], BF16)
+        nc.vector.memset(ones[:], 1.0)
+        eps = keep.tile([P, 1], F32)
+        nc.vector.memset(eps[:], LN_EPS)
+        ident_bf16 = keep.tile([P, P], BF16)
+        make_identity(nc, ident_bf16[:])
+        ident_f32 = keep.tile([P, P], F32)
+        make_identity(nc, ident_f32[:])
+        warm = keep.tile([P, 1], F32)
+        nc.scalar.activation(out=warm[:], in_=eps[:], func=ACT.Sqrt)
+
+        h_loads = []
+        for first in range(0, NODES, LOAD_NODES):
+            count = min(LOAD_NODES, NODES - first)
+            h_load = keep.tile([P, count, D], BF16, name="h_load%d" % first)
+            nc.sync.dma_start(out=h_load[:], in_=h[:, first : first + count, :])
+            h_loads.append(h_load)
+            if first == 0:
+                for j, vec in enumerate((b_l, ln_g, ln_b)):
+                    nc.sync.dma_start(out=rows[0:1, j, :], in_=vec.unsqueeze(0))
         for w, (words, scales) in enumerate(weights):
             for quad in range(4):
                 nc.sync.dma_start(
@@ -64,47 +81,17 @@ def tile_gnnnicheencoder_pa_kernel(
                     in_=words[g].rearrange("p n t -> p (n t)").bitcast(I32),
                 )
 
-        ident_f32 = keep.tile([P, P], F32)
-        make_identity(nc, ident_f32[:])
-        ident_bf16 = keep.tile([P, P], BF16)
-        make_identity(nc, ident_bf16[:])
-        ones = keep.tile([P, P], BF16)
-        nc.vector.memset(ones[:], 1.0)
-        eps = keep.tile([P, 1], F32)
-        nc.vector.memset(eps[:], LN_EPS)
+        def h_node(i):
+            return h_loads[i // LOAD_NODES][:, i % LOAD_NODES, :]
 
-        rows = keep.tile([P, 3, D], BF16)
-        nc.vector.memset(rows[:].bitcast(I32), 0)
-        for j, vec in enumerate((b_l, ln_g, ln_b)):
-            nc.scalar.dma_start(out=rows[0:1, j, :], in_=vec.unsqueeze(0))
-
-        total = [banks.tile([P, K_PASS], F32, tag="bank", name="total%d" % g) for g in range(PASSES)]
-        for i in range(NODES):
-            for g in range(PASSES):
-                nc.tensor.matmul(
-                    out=total[g][:],
-                    lhsT=ident_bf16[:],
-                    rhs=h_sb[:, i, g * K_PASS : (g + 1) * K_PASS],
-                    start=(i == 0),
-                    stop=(i == NODES - 1),
-                )
-
-        bias_ps = banks.tile([P, D], BF16, tag="bank")
-        gain_ps = psum_keep.tile([P, D], BF16)
-        shift_ps = psum_keep.tile([P, D], BF16)
-        for j, spread in enumerate((bias_ps, gain_ps, shift_ps)):
-            for half in range(HALVES):
-                cols = slice(half * N_TILE, (half + 1) * N_TILE)
-                nc.tensor.matmul(out=spread[:, cols], lhsT=ones[:], rhs=rows[:, j, cols], start=True, stop=True)
-        bias_sb = keep.tile([P, D], BF16)
-        nc.scalar.copy(out=bias_sb[:], in_=bias_ps[:])
-
+        h_ts = {}
+        m_ts = {}
         h_side = {}
         m_side = {}
         product = {}
 
-        def transpose_and_quantise_h(i):
-            pairs = h_sb[:, i, :].bitcast(F32)
+        def transpose_h(i):
+            pairs = h_node(i).bitcast(F32)
             flipped = banks.tile([P, PASSES, 2, P], F32, tag="bank")
             for g in range(PASSES):
                 for u in range(2):
@@ -118,31 +105,29 @@ def tile_gnnnicheencoder_pa_kernel(
                 out=h_t[:].bitcast(F32).rearrange("p (g b u) -> p g b u", g=PASSES, u=2),
                 in_=flipped[:].rearrange("p g u b -> p g b u"),
             )
-            h_codes = sides.tile([P, PASSES * P], U32, align_bytes=64)
-            h_plane = sides.tile([P, PASSES * P], U8, align_bytes=64)
-            nc.vector.quantize_mx(out=h_codes[:].bitcast(FP8X4), scales=h_plane[:], in_=h_t[:])
-            h_side[i] = (h_t, h_codes, h_plane)
+            h_ts[i] = h_t
 
-        def mean_of_neighbours(i):
-            h_t = h_side[i][0]
-            m_t = sides.tile([P, D], BF16, align_bytes=64)
-            for g in range(PASSES):
-                cols = slice(g * K_PASS, (g + 1) * K_PASS)
-                nc.vector.scalar_tensor_tensor(
-                    out=m_t[:, cols].rearrange("p (b t) -> p b t", t=PACK),
-                    in0=h_t[:, cols].rearrange("p (b t) -> p b t", t=PACK),
-                    scalar=-1.0 / (NODES - 1),
-                    in1=total_t[g][:].rearrange("p t b -> p b t"),
-                    op0=ALU.mult,
-                    op1=ALU.add,
-                )
-            m_codes = sides.tile([P, PASSES * P], U32, align_bytes=64)
-            m_plane = sides.tile([P, PASSES * P], U8, align_bytes=64)
-            nc.vector.quantize_mx(out=m_codes[:].bitcast(FP8X4), scales=m_plane[:], in_=m_t[:])
-            m_side[i] = (m_codes, m_plane)
+        def mean_of_neighbours(i, g):
+            if g == 0:
+                m_ts[i] = sides.tile([P, D], BF16, align_bytes=64, name="m_t")
+            cols = slice(g * K_PASS, (g + 1) * K_PASS)
+            nc.vector.scalar_tensor_tensor(
+                out=m_ts[i][:, cols].rearrange("p (b t) -> p b t", t=PACK),
+                in0=h_ts[i][:, cols].rearrange("p (b t) -> p b t", t=PACK),
+                scalar=-1.0 / (NODES - 1),
+                in1=total_t[g][:].rearrange("p t b -> p b t"),
+                op0=ALU.mult,
+                op1=ALU.add,
+            )
+
+        def quantise(x_t):
+            codes = sides.tile([P, PASSES * P], U32, align_bytes=64)
+            plane = sides.tile([P, PASSES * P], U8, align_bytes=64)
+            nc.vector.quantize_mx(out=codes[:].bitcast(FP8X4), scales=plane[:], in_=x_t[:])
+            return codes, plane
 
         def multiply(i):
-            operands = (h_side[i][1:], m_side[i])
+            operands = (h_side[i], m_side[i])
             product[i] = []
             for half in range(HALVES):
                 cols = slice(half * N_TILE, (half + 1) * N_TILE)
@@ -161,22 +146,57 @@ def tile_gnnnicheencoder_pa_kernel(
                         )
                 product[i].append(acc)
 
-        for i in range(AHEAD_TRANSPOSE):
-            transpose_and_quantise_h(i)
+        def spread_over_partitions(j, spread):
+            for half in range(HALVES):
+                cols = slice(half * N_TILE, (half + 1) * N_TILE)
+                nc.tensor.matmul(out=spread[:, cols], lhsT=ones[:], rhs=rows[:, j, cols], start=True, stop=True)
+
+        total = [banks.tile([P, K_PASS], F32, tag="bank", name="total%d" % g) for g in range(PASSES)]
+        for i in range(NODES):
+            for g in range(PASSES):
+                nc.tensor.matmul(
+                    out=total[g][:],
+                    lhsT=ident_bf16[:],
+                    rhs=h_node(i)[:, g * K_PASS : (g + 1) * K_PASS],
+                    start=(i == 0),
+                    stop=(i == NODES - 1),
+                )
         total_sb = keep.tile([P, PASSES, PACK, P], F32)
         scaled_copy = (nc.scalar.mul, nc.vector.tensor_scalar_mul)
         for g in range(PASSES):
             scaled_copy[g](total_sb[:, g], total[g][:].rearrange("b (p t) -> b t p", t=PACK), 1.0 / (NODES - 1))
+        transpose_h(0)
         total_t = [psum_keep.tile([P, PACK, P], F32, name="total_t%d" % g) for g in range(PASSES)]
         for g in range(PASSES):
             for t in range(PACK):
                 nc.tensor.transpose(out=total_t[g][:, t, :], in_=total_sb[:, g, t, :], identity=ident_f32[:])
 
-        for i in range(AHEAD_PRODUCTS):
-            mean_of_neighbours(i)
-            multiply(i)
+        h_side[0] = quantise(h_ts[0])
+        transpose_h(1)
+        mean_of_neighbours(0, 0)
+        mean_of_neighbours(0, 1)
+        bias_ps = banks.tile([P, D], BF16, tag="bank")
+        spread_over_partitions(0, bias_ps)
+        bias_sb = keep.tile([P, D], BF16)
+        nc.scalar.copy(out=bias_sb[:], in_=bias_ps[:])
+        h_side[1] = quantise(h_ts[1])
+        m_side[0] = quantise(m_ts[0])
+        multiply(0)
+        mean_of_neighbours(1, 0)
+        mean_of_neighbours(1, 1)
+        gain_ps = psum_keep.tile([P, D], BF16)
+        spread_over_partitions(1, gain_ps)
+        shift_ps = psum_keep.tile([P, D], BF16)
+        spread_over_partitions(2, shift_ps)
+        transpose_h(2)
+        h_side[2] = quantise(h_ts[2])
+        m_side[1] = quantise(m_ts[1])
+        multiply(1)
 
         for i in range(NODES):
+            i_m = i + AHEAD_PRODUCTS if i + AHEAD_PRODUCTS < NODES else None
+            i_h = i + AHEAD_TRANSPOSE if i + AHEAD_TRANSPOSE < NODES else None
+
             c = work.tile([P, D], F32)
             sums = small.tile([P, HALVES], F32)
             for half in range(HALVES):
@@ -190,6 +210,8 @@ def tile_gnnnicheencoder_pa_kernel(
                     op1=ALU.add,
                     accum_out=sums[:, half : half + 1],
                 )
+            if i_m is not None:
+                mean_of_neighbours(i_m, 0)
             neg_mean = small.tile([P, 1], F32)
             nc.vector.tensor_scalar(
                 out=neg_mean[:], in0=sums[:, 0:1], scalar1=sums[:, 1:2], scalar2=-1.0 / D, op0=ALU.add, op1=ALU.mult
@@ -201,27 +223,37 @@ def tile_gnnnicheencoder_pa_kernel(
             )
             std = small.tile([P, 1], F32)
             nc.scalar.activation(out=std[:], in_=sum_sq[:], func=ACT.Sqrt, bias=eps[:], scale=1.0 / D)
+            if i_m is not None:
+                mean_of_neighbours(i_m, 1)
             centred = work.tile([P, D], F32)
             nc.vector.scalar_tensor_tensor(
                 out=centred[:], in0=c[:], scalar=neg_mean[:], in1=gain_ps[:], op0=ALU.add, op1=ALU.mult
             )
-
-            if i + AHEAD_TRANSPOSE < NODES:
-                transpose_and_quantise_h(i + AHEAD_TRANSPOSE)
-            if i + AHEAD_PRODUCTS < NODES:
-                mean_of_neighbours(i + AHEAD_PRODUCTS)
-                multiply(i + AHEAD_PRODUCTS)
-
+            if i_h is not None:
+                transpose_h(i_h)
             rstd = small.tile([P, 1], F32)
             nc.vector.reciprocal(out=rstd[:], in_=std[:])
+            if i_m is not None:
+                m_side[i_m] = quantise(m_ts[i_m])
+                multiply(i_m)
+            if i_h is not None:
+                h_side[i_h] = quantise(h_ts[i_h])
             y = work.tile([P, D], F32)
             nc.vector.scalar_tensor_tensor(
                 out=y[:], in0=centred[:], scalar=rstd[:], in1=shift_ps[:], op0=ALU.mult, op1=ALU.add
             )
-            lift = work.tile([P, D], F32)
-            nc.scalar.activation(out=lift[:], in_=y[:], func=ACT.Relu, scale=-(1.0 - LEAKY_SLOPE))
-            y_plus_h = work.tile([P, D], F32)
-            nc.gpsimd.tensor_tensor(out=y_plus_h[:], in0=y[:], in1=h_sb[:, i, :], op=ALU.add)
+
             result = work.tile([P, D], F32)
-            nc.gpsimd.tensor_tensor(out=result[:], in0=y_plus_h[:], in1=lift[:], op=ALU.add)
+            if i < NODES - 1:
+                lift = work.tile([P, D], F32)
+                nc.scalar.activation(out=lift[:], in_=y[:], func=ACT.Relu, scale=-(1.0 - LEAKY_SLOPE))
+                y_plus_h = work.tile([P, D], F32)
+                nc.gpsimd.tensor_tensor(out=y_plus_h[:], in0=y[:], in1=h_node(i), op=ALU.add)
+                nc.gpsimd.tensor_tensor(out=result[:], in0=y_plus_h[:], in1=lift[:], op=ALU.add)
+            else:
+                leaky = work.tile([P, D], F32)
+                nc.vector.scalar_tensor_tensor(
+                    out=leaky[:], in0=y[:], scalar=LEAKY_SLOPE, in1=y[:], op0=ALU.mult, op1=ALU.max
+                )
+                nc.vector.tensor_tensor(out=result[:], in0=leaky[:], in1=h_node(i), op=ALU.add)
             nc.sync.dma_start(out=out[:, i, :], in_=result[:])

@@ -23,8 +23,10 @@ HALVES = D // N_TILE
 LN_EPS = 1e-5
 LEAKY_SLOPE = 0.01
 LOAD_NODES = 4
-AHEAD_PRODUCTS = 2
-AHEAD_TRANSPOSE = 3
+AHEAD_BIAS = 1
+AHEAD_QUANTISE = 2
+AHEAD_MEAN = 3
+AHEAD_TRANSPOSE = 4
 
 FLOPS = 2 * 2 * P * NODES * D * D
 
@@ -37,11 +39,13 @@ def tile_gnnnicheencoder_pa_kernel(
 
     with ExitStack() as stack:
         keep = stack.enter_context(tc.tile_pool(name="keep", bufs=1))
-        sides = stack.enter_context(tc.tile_pool(name="sides", bufs=4))
+        sides = stack.enter_context(tc.tile_pool(name="sides", bufs=3))
+        swap = stack.enter_context(tc.tile_pool(name="swap", bufs=3))
         work = stack.enter_context(tc.tile_pool(name="work", bufs=3))
         small = stack.enter_context(tc.tile_pool(name="small", bufs=4))
         psum_keep = stack.enter_context(tc.psum_pool(name="psum_keep", bufs=1))
-        banks = stack.enter_context(tc.psum_pool(name="banks", bufs=4))
+        prod = stack.enter_context(tc.psum_pool(name="prod", bufs=4))
+        flip = stack.enter_context(tc.psum_pool(name="flip", bufs=2))
 
         rows = keep.tile([P, 3, D], BF16)
         nc.vector.memset(rows[:].bitcast(I32), 0)
@@ -56,7 +60,7 @@ def tile_gnnnicheencoder_pa_kernel(
         ident_f32 = keep.tile([P, P], F32)
         make_identity(nc, ident_f32[:])
         warm = keep.tile([P, 1], F32)
-        nc.scalar.activation(out=warm[:], in_=eps[:], func=ACT.Sqrt)
+        nc.scalar.activation(out=warm[:], in_=eps[:], func=ACT.Abs_reciprocal_sqrt)
 
         h_loads = []
         for first in range(0, NODES, LOAD_NODES):
@@ -84,57 +88,52 @@ def tile_gnnnicheencoder_pa_kernel(
         def h_node(i):
             return h_loads[i // LOAD_NODES][:, i % LOAD_NODES, :]
 
-        h_ts = {}
-        m_ts = {}
-        h_side = {}
-        m_side = {}
+        flipped = {}
+        x_ts = {}
+        sides_of = {}
         product = {}
+        cs, neg_means, rstds, centreds, ys, lifts = {}, {}, {}, {}, {}, {}
 
-        def transpose_h(i):
-            pairs = h_node(i).bitcast(F32)
-            flipped = banks.tile([P, PASSES, 2, P], F32, tag="bank")
+        def transpose_h(j):
+            pairs = h_node(j).bitcast(F32)
+            flipped[j] = flip.tile([P, PASSES, P, 2], F32, tag="flip", name="flipped")
             for g in range(PASSES):
                 for u in range(2):
                     nc.tensor.transpose(
-                        out=flipped[:, g, u, :],
+                        out=flipped[j][:, g, :, u],
                         in_=pairs[:, 256 * g + u : 256 * (g + 1) : 2],
                         identity=ident_f32[:],
                     )
-            h_t = sides.tile([P, D], BF16, align_bytes=64)
-            nc.scalar.copy(
-                out=h_t[:].bitcast(F32).rearrange("p (g b u) -> p g b u", g=PASSES, u=2),
-                in_=flipped[:].rearrange("p g u b -> p g b u"),
-            )
-            h_ts[i] = h_t
+            x_ts[j] = swap.tile([P, 2, D], BF16, tag="swap", align_bytes=64, name="x_t")
+            nc.scalar.copy(out=x_ts[j][:, 0, :].bitcast(F32), in_=flipped[j][:].rearrange("p g b u -> p (g b u)"))
 
-        def mean_of_neighbours(i, g):
-            if g == 0:
-                m_ts[i] = sides.tile([P, D], BF16, align_bytes=64, name="m_t")
-            cols = slice(g * K_PASS, (g + 1) * K_PASS)
+        def mean_of_neighbours(j):
             nc.vector.scalar_tensor_tensor(
-                out=m_ts[i][:, cols].rearrange("p (b t) -> p b t", t=PACK),
-                in0=h_ts[i][:, cols].rearrange("p (b t) -> p b t", t=PACK),
+                out=x_ts[j][:, 1, :],
+                in0=flipped[j][:].rearrange("p g b u -> p (g b u)").bitcast(BF16),
                 scalar=-1.0 / (NODES - 1),
-                in1=total_t[g][:].rearrange("p t b -> p b t"),
+                in1=total_t[:],
                 op0=ALU.mult,
                 op1=ALU.add,
             )
 
-        def quantise(x_t):
-            codes = sides.tile([P, PASSES * P], U32, align_bytes=64)
-            plane = sides.tile([P, PASSES * P], U8, align_bytes=64)
-            nc.vector.quantize_mx(out=codes[:].bitcast(FP8X4), scales=plane[:], in_=x_t[:])
-            return codes, plane
+        def quantise(j):
+            codes = sides.tile([P, 2 * PASSES * P], U32, align_bytes=64)
+            plane = sides.tile([P, 2 * PASSES * P], U8, align_bytes=64)
+            nc.vector.quantize_mx(
+                out=codes[:].bitcast(FP8X4), scales=plane[:], in_=x_ts[j][:].rearrange("p w d -> p (w d)")
+            )
+            sides_of[j] = (codes, plane)
 
-        def multiply(i):
-            operands = (h_side[i], m_side[i])
-            product[i] = []
+        def multiply(j):
+            codes, plane = sides_of[j]
+            product[j] = []
             for half in range(HALVES):
                 cols = slice(half * N_TILE, (half + 1) * N_TILE)
-                acc = banks.tile([P, N_TILE], F32, tag="bank")
-                for w, (codes, plane) in enumerate(operands):
+                acc = prod.tile([P, N_TILE], F32, tag="prod")
+                for w in range(2):
                     for g in range(PASSES):
-                        graphs = slice(g * P, (g + 1) * P)
+                        graphs = slice((w * PASSES + g) * P, (w * PASSES + g + 1) * P)
                         nc.tensor.matmul_mx(
                             out=acc[:],
                             lhsT=codes[:, graphs].bitcast(FP8X4),
@@ -144,14 +143,80 @@ def tile_gnnnicheencoder_pa_kernel(
                             start=(w == 0 and g == 0),
                             stop=(w == 1 and g == PASSES - 1),
                         )
-                product[i].append(acc)
+                product[j].append(acc)
 
         def spread_over_partitions(j, spread):
             for half in range(HALVES):
                 cols = slice(half * N_TILE, (half + 1) * N_TILE)
                 nc.tensor.matmul(out=spread[:, cols], lhsT=ones[:], rhs=rows[:, j, cols], start=True, stop=True)
 
-        total = [banks.tile([P, K_PASS], F32, tag="bank", name="total%d" % g) for g in range(PASSES)]
+        def add_bias(i):
+            cs[i] = work.tile([P, D], F32, name="c")
+            sums = small.tile([P, HALVES], F32)
+            for half in range(HALVES):
+                cols = slice(half * N_TILE, (half + 1) * N_TILE)
+                nc.vector.scalar_tensor_tensor(
+                    out=cs[i][:, cols],
+                    in0=product[i][half][:],
+                    scalar=1.0,
+                    in1=bias_sb[:, cols],
+                    op0=ALU.mult,
+                    op1=ALU.add,
+                    accum_out=sums[:, half : half + 1],
+                )
+            neg_means[i] = small.tile([P, 1], F32, name="neg_mean")
+            scaled_sums = small.tile([P, HALVES], F32)
+            nc.scalar.activation(
+                out=scaled_sums[:], in_=sums[:], func=ACT.Copy, scale=-1.0 / D, accum_out=neg_means[i][:]
+            )
+            squares = work.tile([P, D], BF16)
+            sum_sq = small.tile([P, 1], F32)
+            nc.scalar.activation(
+                out=squares[:], in_=cs[i][:], func=ACT.Square, bias=neg_means[i][:], scale=1.0, accum_out=sum_sq[:]
+            )
+            rstds[i] = small.tile([P, 1], F32, name="rstd")
+            nc.scalar.activation(
+                out=rstds[i][:], in_=sum_sq[:], func=ACT.Abs_reciprocal_sqrt, bias=eps[:], scale=1.0 / D
+            )
+
+        def centre_and_gain(i):
+            centreds[i] = work.tile([P, D], F32, name="centred")
+            nc.vector.scalar_tensor_tensor(
+                out=centreds[i][:], in0=cs[i][:], scalar=neg_means[i][:], in1=gain_ps[:], op0=ALU.add, op1=ALU.mult
+            )
+
+        def scale_and_shift(i):
+            ys[i] = work.tile([P, D], F32, name="y")
+            nc.vector.scalar_tensor_tensor(
+                out=ys[i][:], in0=centreds[i][:], scalar=rstds[i][:], in1=shift_ps[:], op0=ALU.mult, op1=ALU.add
+            )
+
+        def lift_negatives(i, cols):
+            lifts[i] = work.tile([P, D], F32, name="lift")
+            nc.scalar.activation(
+                out=lifts[i][:, cols], in_=ys[i][:, cols], func=ACT.Relu, scale=-(1.0 - LEAKY_SLOPE)
+            )
+
+        def finish_on_gpsimd(i, cols):
+            y_plus_h = swap.tile([P, D], F32, tag="swap", align_bytes=64)
+            nc.gpsimd.tensor_tensor(out=y_plus_h[:, cols], in0=ys[i][:, cols], in1=h_node(i)[:, cols], op=ALU.add)
+            result = work.tile([P, D], F32)
+            nc.gpsimd.tensor_tensor(out=result[:, cols], in0=y_plus_h[:, cols], in1=lifts[i][:, cols], op=ALU.add)
+            nc.sync.dma_start(out=out[:, i, cols], in_=result[:, cols])
+
+        def leaky_on_vector(i, cols):
+            leaky = work.tile([P, N_TILE], F32)
+            nc.vector.scalar_tensor_tensor(
+                out=leaky[:], in0=ys[i][:, cols], scalar=LEAKY_SLOPE, in1=ys[i][:, cols], op0=ALU.mult, op1=ALU.max
+            )
+            return leaky
+
+        def add_h_on_vector(i, cols, leaky):
+            result_v = work.tile([P, N_TILE], F32)
+            nc.vector.tensor_tensor(out=result_v[:], in0=leaky[:], in1=h_node(i)[:, cols], op=ALU.add)
+            nc.sync.dma_start(out=out[:, i, cols], in_=result_v[:])
+
+        total = [prod.tile([P, K_PASS], F32, tag="prod", name="total%d" % g) for g in range(PASSES)]
         for i in range(NODES):
             for g in range(PASSES):
                 nc.tensor.matmul(
@@ -161,99 +226,58 @@ def tile_gnnnicheencoder_pa_kernel(
                     start=(i == 0),
                     stop=(i == NODES - 1),
                 )
+        transpose_h(0)
+        transpose_h(1)
         total_sb = keep.tile([P, PASSES, PACK, P], F32)
         scaled_copy = (nc.scalar.mul, nc.vector.tensor_scalar_mul)
         for g in range(PASSES):
             scaled_copy[g](total_sb[:, g], total[g][:].rearrange("b (p t) -> b t p", t=PACK), 1.0 / (NODES - 1))
-        transpose_h(0)
-        total_t = [psum_keep.tile([P, PACK, P], F32, name="total_t%d" % g) for g in range(PASSES)]
+        total_ps = [prod.tile([P, P, PACK], F32, tag="prod", name="total_ps%d" % g) for g in range(PASSES)]
         for g in range(PASSES):
             for t in range(PACK):
-                nc.tensor.transpose(out=total_t[g][:, t, :], in_=total_sb[:, g, t, :], identity=ident_f32[:])
-
-        h_side[0] = quantise(h_ts[0])
-        transpose_h(1)
-        mean_of_neighbours(0, 0)
-        mean_of_neighbours(0, 1)
-        bias_ps = banks.tile([P, D], BF16, tag="bank")
+                nc.tensor.transpose(out=total_ps[g][:, :, t], in_=total_sb[:, g, t, :], identity=ident_f32[:])
+        total_t = keep.tile([P, D], F32)
+        plain_copy = (nc.vector.tensor_copy, nc.scalar.copy)
+        for g in range(PASSES):
+            plain_copy[g](
+                out=total_t[:, g * K_PASS : (g + 1) * K_PASS], in_=total_ps[g][:].rearrange("p b t -> p (b t)")
+            )
+        bias_ps = prod.tile([P, D], BF16, tag="prod")
         spread_over_partitions(0, bias_ps)
         bias_sb = keep.tile([P, D], BF16)
         nc.scalar.copy(out=bias_sb[:], in_=bias_ps[:])
-        h_side[1] = quantise(h_ts[1])
-        m_side[0] = quantise(m_ts[0])
-        multiply(0)
-        mean_of_neighbours(1, 0)
-        mean_of_neighbours(1, 1)
         gain_ps = psum_keep.tile([P, D], BF16)
         spread_over_partitions(1, gain_ps)
         shift_ps = psum_keep.tile([P, D], BF16)
         spread_over_partitions(2, shift_ps)
-        transpose_h(2)
-        h_side[2] = quantise(h_ts[2])
-        m_side[1] = quantise(m_ts[1])
-        multiply(1)
 
-        for i in range(NODES):
-            i_m = i + AHEAD_PRODUCTS if i + AHEAD_PRODUCTS < NODES else None
-            i_h = i + AHEAD_TRANSPOSE if i + AHEAD_TRANSPOSE < NODES else None
+        halves = [slice(half * N_TILE, (half + 1) * N_TILE) for half in range(HALVES)]
 
-            c = work.tile([P, D], F32)
-            sums = small.tile([P, HALVES], F32)
-            for half in range(HALVES):
-                cols = slice(half * N_TILE, (half + 1) * N_TILE)
-                nc.vector.scalar_tensor_tensor(
-                    out=c[:, cols],
-                    in0=product[i][half][:],
-                    scalar=1.0,
-                    in1=bias_sb[:, cols],
-                    op0=ALU.mult,
-                    op1=ALU.add,
-                    accum_out=sums[:, half : half + 1],
-                )
-            if i_m is not None:
-                mean_of_neighbours(i_m, 0)
-            neg_mean = small.tile([P, 1], F32)
-            nc.vector.tensor_scalar(
-                out=neg_mean[:], in0=sums[:, 0:1], scalar1=sums[:, 1:2], scalar2=-1.0 / D, op0=ALU.add, op1=ALU.mult
-            )
-            squares = work.tile([P, D], BF16)
-            sum_sq = small.tile([P, 1], F32)
-            nc.scalar.activation(
-                out=squares[:], in_=c[:], func=ACT.Square, bias=neg_mean[:], scale=1.0, accum_out=sum_sq[:]
-            )
-            std = small.tile([P, 1], F32)
-            nc.scalar.activation(out=std[:], in_=sum_sq[:], func=ACT.Sqrt, bias=eps[:], scale=1.0 / D)
-            if i_m is not None:
-                mean_of_neighbours(i_m, 1)
-            centred = work.tile([P, D], F32)
-            nc.vector.scalar_tensor_tensor(
-                out=centred[:], in0=c[:], scalar=neg_mean[:], in1=gain_ps[:], op0=ALU.add, op1=ALU.mult
-            )
-            if i_h is not None:
-                transpose_h(i_h)
-            rstd = small.tile([P, 1], F32)
-            nc.vector.reciprocal(out=rstd[:], in_=std[:])
-            if i_m is not None:
-                m_side[i_m] = quantise(m_ts[i_m])
-                multiply(i_m)
-            if i_h is not None:
-                h_side[i_h] = quantise(h_ts[i_h])
-            y = work.tile([P, D], F32)
-            nc.vector.scalar_tensor_tensor(
-                out=y[:], in0=centred[:], scalar=rstd[:], in1=shift_ps[:], op0=ALU.mult, op1=ALU.add
-            )
+        def gpsimd_cols(i):
+            return slice(0, D) if i < NODES - 2 else halves[0]
 
-            result = work.tile([P, D], F32)
-            if i < NODES - 1:
-                lift = work.tile([P, D], F32)
-                nc.scalar.activation(out=lift[:], in_=y[:], func=ACT.Relu, scale=-(1.0 - LEAKY_SLOPE))
-                y_plus_h = work.tile([P, D], F32)
-                nc.gpsimd.tensor_tensor(out=y_plus_h[:], in0=y[:], in1=h_node(i), op=ALU.add)
-                nc.gpsimd.tensor_tensor(out=result[:], in0=y_plus_h[:], in1=lift[:], op=ALU.add)
-            else:
-                leaky = work.tile([P, D], F32)
-                nc.vector.scalar_tensor_tensor(
-                    out=leaky[:], in0=y[:], scalar=LEAKY_SLOPE, in1=y[:], op0=ALU.mult, op1=ALU.max
-                )
-                nc.vector.tensor_tensor(out=result[:], in0=leaky[:], in1=h_node(i), op=ALU.add)
-            nc.sync.dma_start(out=out[:, i, :], in_=result[:])
+        with tc.manual_schedule(engines={mybir.EngineType.DVE}):
+            for i in range(-AHEAD_MEAN, NODES):
+                if 0 <= i + AHEAD_QUANTISE < NODES:
+                    quantise(i + AHEAD_QUANTISE)
+                    multiply(i + AHEAD_QUANTISE)
+                if i >= 1:
+                    finish_on_gpsimd(i - 1, gpsimd_cols(i - 1))
+                if 0 <= i + AHEAD_BIAS < NODES:
+                    add_bias(i + AHEAD_BIAS)
+                if 2 <= i + AHEAD_TRANSPOSE < NODES:
+                    transpose_h(i + AHEAD_TRANSPOSE)
+                if i >= 0:
+                    centre_and_gain(i)
+                if i + AHEAD_MEAN < NODES:
+                    mean_of_neighbours(i + AHEAD_MEAN)
+                if i == NODES - 1:
+                    leaky_before = leaky_on_vector(i - 1, halves[1])
+                if i >= 0:
+                    scale_and_shift(i)
+                    if i < NODES - 1:
+                        lift_negatives(i, gpsimd_cols(i))
+            add_h_on_vector(NODES - 2, halves[1], leaky_before)
+            leaky_last = [leaky_on_vector(NODES - 1, cols) for cols in halves]
+            for cols, leaky in zip(halves, leaky_last):
+                add_h_on_vector(NODES - 1, cols, leaky)

@@ -23,10 +23,9 @@ HALVES = D // N_TILE
 LN_EPS = 1e-5
 LEAKY_SLOPE = 0.01
 LOAD_NODES = 4
-AHEAD_BIAS = 1
-AHEAD_QUANTISE = 2
-AHEAD_MEAN = 3
-AHEAD_TRANSPOSE = 4
+AHEAD_QUANTISE = 1
+AHEAD_MEAN = 2
+AHEAD_TRANSPOSE = 3
 
 FLOPS = 2 * 2 * P * NODES * D * D
 
@@ -92,7 +91,9 @@ def tile_gnnnicheencoder_pa_kernel(
         x_ts = {}
         sides_of = {}
         product = {}
-        cs, neg_means, rstds, centreds, ys, lifts = {}, {}, {}, {}, {}, {}
+        cs, sums_of, neg_means, rstds, centreds, ys, lifts = {}, {}, {}, {}, {}, {}, {}
+        halves = [slice(half * N_TILE, (half + 1) * N_TILE) for half in range(HALVES)]
+        whole = slice(0, D)
 
         def transpose_h(j):
             pairs = h_node(j).bitcast(F32)
@@ -107,12 +108,13 @@ def tile_gnnnicheencoder_pa_kernel(
             x_ts[j] = swap.tile([P, 2, D], BF16, tag="swap", align_bytes=64, name="x_t")
             nc.scalar.copy(out=x_ts[j][:, 0, :].bitcast(F32), in_=flipped[j][:].rearrange("p g b u -> p (g b u)"))
 
-        def mean_of_neighbours(j):
+        def mean_of_neighbours(j, g):
+            cols = slice(g * K_PASS, (g + 1) * K_PASS)
             nc.vector.scalar_tensor_tensor(
-                out=x_ts[j][:, 1, :],
-                in0=flipped[j][:].rearrange("p g b u -> p (g b u)").bitcast(BF16),
+                out=x_ts[j][:, 1, cols],
+                in0=flipped[j][:, g].rearrange("p b u -> p (b u)").bitcast(BF16),
                 scalar=-1.0 / (NODES - 1),
-                in1=total_t[:],
+                in1=total_t[:, cols],
                 op0=ALU.mult,
                 op1=ALU.add,
             )
@@ -150,24 +152,25 @@ def tile_gnnnicheencoder_pa_kernel(
                 cols = slice(half * N_TILE, (half + 1) * N_TILE)
                 nc.tensor.matmul(out=spread[:, cols], lhsT=ones[:], rhs=rows[:, j, cols], start=True, stop=True)
 
-        def add_bias(i):
-            cs[i] = work.tile([P, D], F32, name="c")
-            sums = small.tile([P, HALVES], F32)
-            for half in range(HALVES):
-                cols = slice(half * N_TILE, (half + 1) * N_TILE)
-                nc.vector.scalar_tensor_tensor(
-                    out=cs[i][:, cols],
-                    in0=product[i][half][:],
-                    scalar=1.0,
-                    in1=bias_sb[:, cols],
-                    op0=ALU.mult,
-                    op1=ALU.add,
-                    accum_out=sums[:, half : half + 1],
-                )
+        def add_bias(i, half):
+            if half == 0:
+                cs[i] = work.tile([P, D], F32, name="c")
+                sums_of[i] = small.tile([P, HALVES], F32, name="sums")
+            nc.vector.scalar_tensor_tensor(
+                out=cs[i][:, halves[half]],
+                in0=product[i][half][:],
+                scalar=1.0,
+                in1=bias_sb[:, halves[half]],
+                op0=ALU.mult,
+                op1=ALU.add,
+                accum_out=sums_of[i][:, half : half + 1],
+            )
+
+        def statistics(i):
             neg_means[i] = small.tile([P, 1], F32, name="neg_mean")
             scaled_sums = small.tile([P, HALVES], F32)
             nc.scalar.activation(
-                out=scaled_sums[:], in_=sums[:], func=ACT.Copy, scale=-1.0 / D, accum_out=neg_means[i][:]
+                out=scaled_sums[:], in_=sums_of[i][:], func=ACT.Copy, scale=-1.0 / D, accum_out=neg_means[i][:]
             )
             squares = work.tile([P, D], BF16)
             sum_sq = small.tile([P, 1], F32)
@@ -179,16 +182,20 @@ def tile_gnnnicheencoder_pa_kernel(
                 out=rstds[i][:], in_=sum_sq[:], func=ACT.Abs_reciprocal_sqrt, bias=eps[:], scale=1.0 / D
             )
 
-        def centre_and_gain(i):
-            centreds[i] = work.tile([P, D], F32, name="centred")
+        def centre_and_gain(i, cols):
+            if cols.start == 0:
+                centreds[i] = work.tile([P, D], F32, name="centred")
             nc.vector.scalar_tensor_tensor(
-                out=centreds[i][:], in0=cs[i][:], scalar=neg_means[i][:], in1=gain_ps[:], op0=ALU.add, op1=ALU.mult
+                out=centreds[i][:, cols], in0=cs[i][:, cols], scalar=neg_means[i][:], in1=gain_ps[:, cols],
+                op0=ALU.add, op1=ALU.mult,
             )
 
-        def scale_and_shift(i):
-            ys[i] = work.tile([P, D], F32, name="y")
+        def scale_and_shift(i, cols):
+            if cols.start == 0:
+                ys[i] = work.tile([P, D], F32, name="y")
             nc.vector.scalar_tensor_tensor(
-                out=ys[i][:], in0=centreds[i][:], scalar=rstds[i][:], in1=shift_ps[:], op0=ALU.mult, op1=ALU.add
+                out=ys[i][:, cols], in0=centreds[i][:, cols], scalar=rstds[i][:], in1=shift_ps[:, cols],
+                op0=ALU.mult, op1=ALU.add,
             )
 
         def lift_negatives(i, cols):
@@ -203,6 +210,15 @@ def tile_gnnnicheencoder_pa_kernel(
             result = work.tile([P, D], F32)
             nc.gpsimd.tensor_tensor(out=result[:, cols], in0=y_plus_h[:, cols], in1=lifts[i][:, cols], op=ALU.add)
             nc.sync.dma_start(out=out[:, i, cols], in_=result[:, cols])
+
+        def finish_in_halves_on_gpsimd(i):
+            y_plus_h = swap.tile([P, D], F32, tag="swap", align_bytes=64)
+            for cols in halves:
+                nc.gpsimd.tensor_tensor(out=y_plus_h[:, cols], in0=ys[i][:, cols], in1=h_node(i)[:, cols], op=ALU.add)
+            result = work.tile([P, D], F32)
+            for cols in halves:
+                nc.gpsimd.tensor_tensor(out=result[:, cols], in0=y_plus_h[:, cols], in1=lifts[i][:, cols], op=ALU.add)
+                nc.sync.dma_start(out=out[:, i, cols], in_=result[:, cols])
 
         def leaky_on_vector(i, cols):
             leaky = work.tile([P, N_TILE], F32)
@@ -251,33 +267,38 @@ def tile_gnnnicheencoder_pa_kernel(
         shift_ps = psum_keep.tile([P, D], BF16)
         spread_over_partitions(2, shift_ps)
 
-        halves = [slice(half * N_TILE, (half + 1) * N_TILE) for half in range(HALVES)]
-
-        def gpsimd_cols(i):
-            return slice(0, D) if i < NODES - 2 else halves[0]
+        LAST = NODES - 1
 
         with tc.manual_schedule(engines={mybir.EngineType.DVE}):
-            for i in range(-AHEAD_MEAN, NODES):
-                if 0 <= i + AHEAD_QUANTISE < NODES:
+            for i in range(-AHEAD_MEAN, LAST):
+                if 0 <= i + AHEAD_QUANTISE:
                     quantise(i + AHEAD_QUANTISE)
                     multiply(i + AHEAD_QUANTISE)
                 if i >= 1:
-                    finish_on_gpsimd(i - 1, gpsimd_cols(i - 1))
-                if 0 <= i + AHEAD_BIAS < NODES:
-                    add_bias(i + AHEAD_BIAS)
+                    finish_on_gpsimd(i - 1, whole)
+                if i >= 0:
+                    add_bias(i, 0)
+                    add_bias(i, 1)
+                    statistics(i)
                 if 2 <= i + AHEAD_TRANSPOSE < NODES:
                     transpose_h(i + AHEAD_TRANSPOSE)
+                for step in range(2):
+                    if i + AHEAD_MEAN < NODES:
+                        mean_of_neighbours(i + AHEAD_MEAN, step)
+                    elif i == LAST - 1:
+                        add_bias(LAST, step)
+                    if step == 0 and i >= 0:
+                        centre_and_gain(i, whole)
+                if i == LAST - 1:
+                    statistics(LAST)
                 if i >= 0:
-                    centre_and_gain(i)
-                if i + AHEAD_MEAN < NODES:
-                    mean_of_neighbours(i + AHEAD_MEAN)
-                if i == NODES - 1:
-                    leaky_before = leaky_on_vector(i - 1, halves[1])
-                if i >= 0:
-                    scale_and_shift(i)
-                    if i < NODES - 1:
-                        lift_negatives(i, gpsimd_cols(i))
-            add_h_on_vector(NODES - 2, halves[1], leaky_before)
-            leaky_last = [leaky_on_vector(NODES - 1, cols) for cols in halves]
+                    scale_and_shift(i, whole)
+                    lift_negatives(i, whole)
+            finish_in_halves_on_gpsimd(LAST - 1)
+            for cols in halves:
+                centre_and_gain(LAST, cols)
+            for cols in halves:
+                scale_and_shift(LAST, cols)
+            leaky_last = [leaky_on_vector(LAST, cols) for cols in halves]
             for cols, leaky in zip(halves, leaky_last):
-                add_h_on_vector(NODES - 1, cols, leaky)
+                add_h_on_vector(LAST, cols, leaky)

@@ -248,15 +248,25 @@ def tile_gnnnicheencoder_pa_kernel(
         scaled_copy = (nc.scalar.mul, nc.vector.tensor_scalar_mul)
         for g in range(PASSES):
             scaled_copy[g](total_sb[:, g], total[g][:].rearrange("b (p t) -> b t p", t=PACK), 1.0 / (NODES - 1))
-        total_ps = [prod.tile([P, P, PACK], F32, tag="prod", name="total_ps%d" % g) for g in range(PASSES)]
+        total_ps = [prod.tile([P, PACK, P], F32, tag="prod", name="total_ps%d" % g) for g in range(PASSES)]
         for g in range(PASSES):
             for t in range(PACK):
-                nc.tensor.transpose(out=total_ps[g][:, :, t], in_=total_sb[:, g, t, :], identity=ident_f32[:])
-        total_t = keep.tile([P, D], F32)
-        plain_copy = (nc.vector.tensor_copy, nc.scalar.copy)
+                nc.tensor.transpose(out=total_ps[g][:, t, :], in_=total_sb[:, g, t, :], identity=ident_f32[:])
         for g in range(PASSES):
-            plain_copy[g](
-                out=total_t[:, g * K_PASS : (g + 1) * K_PASS], in_=total_ps[g][:].rearrange("p b t -> p (b t)")
+            cols = slice(g * K_PASS, (g + 1) * K_PASS)
+            nc.vector.scalar_tensor_tensor(
+                out=x_ts[0][:, 1, cols].rearrange("p (b t) -> p b t", t=PACK),
+                in0=x_ts[0][:, 0, cols].rearrange("p (b t) -> p b t", t=PACK),
+                scalar=-1.0 / (NODES - 1),
+                in1=total_ps[g][:].rearrange("p t b -> p b t"),
+                op0=ALU.mult,
+                op1=ALU.add,
+            )
+        total_t = keep.tile([P, D], F32)
+        for g in range(PASSES):
+            nc.scalar.copy(
+                out=total_t[:, g * K_PASS : (g + 1) * K_PASS].rearrange("p (b t) -> p b t", t=PACK),
+                in_=total_ps[g][:].rearrange("p t b -> p b t"),
             )
         bias_ps = prod.tile([P, D], BF16, tag="prod")
         spread_over_partitions(0, bias_ps)
@@ -270,7 +280,7 @@ def tile_gnnnicheencoder_pa_kernel(
         LAST = NODES - 1
 
         with tc.manual_schedule(engines={mybir.EngineType.DVE}):
-            for i in range(-AHEAD_MEAN, LAST):
+            for i in range(-AHEAD_QUANTISE, LAST):
                 if 0 <= i + AHEAD_QUANTISE:
                     quantise(i + AHEAD_QUANTISE)
                     multiply(i + AHEAD_QUANTISE)

@@ -23,6 +23,8 @@ HALVES = D // N_TILE
 LN_EPS = 1e-5
 LEAKY_SLOPE = 0.01
 LOAD_NODES = 4
+EARLY_NODES = 2
+LATER_IN_BANK = ("gain", "shift")
 AHEAD_QUANTISE = 1
 AHEAD_MEAN = 2
 AHEAD_TRANSPOSE = 3
@@ -97,19 +99,36 @@ def tile_gnnnicheencoder_pa_kernel(
 
         def transpose_h(j):
             pairs = h_node(j).bitcast(F32)
-            flipped[j] = flip.tile([P, PASSES, P, 2], F32, tag="flip", name="flipped")
+            early = j < EARLY_NODES
+            flipped[j] = flip.tile([P, PASSES, 2, P] if early else [P, PASSES, P, 2], F32, tag="flip", name="flipped")
             for g in range(PASSES):
                 for u in range(2):
                     nc.tensor.transpose(
-                        out=flipped[j][:, g, :, u],
+                        out=flipped[j][:, g, u, :] if early else flipped[j][:, g, :, u],
                         in_=pairs[:, 256 * g + u : 256 * (g + 1) : 2],
                         identity=ident_f32[:],
                     )
             x_ts[j] = swap.tile([P, 2, D], BF16, tag="swap", align_bytes=64, name="x_t")
-            nc.scalar.copy(out=x_ts[j][:, 0, :].bitcast(F32), in_=flipped[j][:].rearrange("p g b u -> p (g b u)"))
+            if early:
+                nc.scalar.copy(
+                    out=x_ts[j][:, 0, :].bitcast(F32).rearrange("p (g b u) -> p g b u", g=PASSES, u=2),
+                    in_=flipped[j][:].rearrange("p g u b -> p g b u"),
+                )
+            else:
+                nc.scalar.copy(out=x_ts[j][:, 0, :].bitcast(F32), in_=flipped[j][:].rearrange("p g b u -> p (g b u)"))
 
         def mean_of_neighbours(j, g):
             cols = slice(g * K_PASS, (g + 1) * K_PASS)
+            if j < EARLY_NODES:
+                nc.vector.scalar_tensor_tensor(
+                    out=x_ts[j][:, 1, cols].rearrange("p (b t) -> p b t", t=PACK),
+                    in0=x_ts[j][:, 0, cols].rearrange("p (b t) -> p b t", t=PACK),
+                    scalar=-1.0 / (NODES - 1),
+                    in1=total_ps[g][:].rearrange("p t b -> p b t"),
+                    op0=ALU.mult,
+                    op1=ALU.add,
+                )
+                return
             nc.vector.scalar_tensor_tensor(
                 out=x_ts[j][:, 1, cols],
                 in0=flipped[j][:, g].rearrange("p b u -> p (b u)").bitcast(BF16),
@@ -248,20 +267,12 @@ def tile_gnnnicheencoder_pa_kernel(
         scaled_copy = (nc.scalar.mul, nc.vector.tensor_scalar_mul)
         for g in range(PASSES):
             scaled_copy[g](total_sb[:, g], total[g][:].rearrange("b (p t) -> b t p", t=PACK), 1.0 / (NODES - 1))
-        total_ps = [prod.tile([P, PACK, P], F32, tag="prod", name="total_ps%d" % g) for g in range(PASSES)]
+        total_ps = [psum_keep.tile([P, PACK, P], F32, tag=LATER_IN_BANK[g], name="total_ps%d" % g) for g in range(PASSES)]
         for g in range(PASSES):
             for t in range(PACK):
                 nc.tensor.transpose(out=total_ps[g][:, t, :], in_=total_sb[:, g, t, :], identity=ident_f32[:])
         for g in range(PASSES):
-            cols = slice(g * K_PASS, (g + 1) * K_PASS)
-            nc.vector.scalar_tensor_tensor(
-                out=x_ts[0][:, 1, cols].rearrange("p (b t) -> p b t", t=PACK),
-                in0=x_ts[0][:, 0, cols].rearrange("p (b t) -> p b t", t=PACK),
-                scalar=-1.0 / (NODES - 1),
-                in1=total_ps[g][:].rearrange("p t b -> p b t"),
-                op0=ALU.mult,
-                op1=ALU.add,
-            )
+            mean_of_neighbours(0, g)
         total_t = keep.tile([P, D], F32)
         for g in range(PASSES):
             nc.scalar.copy(
@@ -272,10 +283,6 @@ def tile_gnnnicheencoder_pa_kernel(
         spread_over_partitions(0, bias_ps)
         bias_sb = keep.tile([P, D], BF16)
         nc.scalar.copy(out=bias_sb[:], in_=bias_ps[:])
-        gain_ps = psum_keep.tile([P, D], BF16)
-        spread_over_partitions(1, gain_ps)
-        shift_ps = psum_keep.tile([P, D], BF16)
-        spread_over_partitions(2, shift_ps)
 
         LAST = NODES - 1
 
@@ -299,6 +306,11 @@ def tile_gnnnicheencoder_pa_kernel(
                         add_bias(LAST, step)
                     if step == 0 and i >= 0:
                         centre_and_gain(i, whole)
+                if i + AHEAD_MEAN == EARLY_NODES - 1:
+                    gain_ps = psum_keep.tile([P, D], BF16, tag=LATER_IN_BANK[0])
+                    spread_over_partitions(1, gain_ps)
+                    shift_ps = psum_keep.tile([P, D], BF16, tag=LATER_IN_BANK[1])
+                    spread_over_partitions(2, shift_ps)
                 if i == LAST - 1:
                     statistics(LAST)
                 if i >= 0:

@@ -13,7 +13,10 @@ ALU = mybir.AluOpType
 ACT = mybir.ActivationFunctionType
 
 P = 128
+GRAPHS = 128
 NODES = 17
+ROWS = GRAPHS * NODES
+TILES = ROWS // P
 D = 1024
 PACK = 4
 K_PASS = P * PACK
@@ -22,14 +25,12 @@ N_TILE = 512
 HALVES = D // N_TILE
 LN_EPS = 1e-5
 LEAKY_SLOPE = 0.01
-LOAD_NODES = 4
-EARLY_NODES = 2
-LATER_IN_BANK = ("gain", "shift")
-AHEAD_QUANTISE = 1
-AHEAD_MEAN = 2
-AHEAD_TRANSPOSE = 3
+GROUP = (P // NODES) * NODES
+GROUPS = -(-ROWS // GROUP)
+LAST_WINDOW = ROWS - P
+MEAN_PITCH = 120
 
-FLOPS = 2 * 2 * P * NODES * D * D
+FLOPS = 2 * 2 * ROWS * D * D
 
 
 def tile_gnnnicheencoder_pa_kernel(
@@ -37,59 +38,98 @@ def tile_gnnnicheencoder_pa_kernel(
 ):
     nc = tc.nc
     weights = ((W_r_words, W_r_scales), (W_l_words, W_l_scales))
+    h_rows = h.rearrange("b n d -> (b n) d")
+    out_rows = out.rearrange("b n d -> (b n) d")
 
     with ExitStack() as stack:
         keep = stack.enter_context(tc.tile_pool(name="keep", bufs=1))
         sides = stack.enter_context(tc.tile_pool(name="sides", bufs=3))
-        swap = stack.enter_context(tc.tile_pool(name="swap", bufs=3))
+        swap = stack.enter_context(tc.tile_pool(name="swap", bufs=4))
         work = stack.enter_context(tc.tile_pool(name="work", bufs=3))
         small = stack.enter_context(tc.tile_pool(name="small", bufs=4))
         psum_keep = stack.enter_context(tc.psum_pool(name="psum_keep", bufs=1))
         prod = stack.enter_context(tc.psum_pool(name="prod", bufs=4))
-        flip = stack.enter_context(tc.psum_pool(name="flip", bufs=2))
+        flip = stack.enter_context(tc.psum_pool(name="flip", bufs=1))
+        mean = stack.enter_context(tc.psum_pool(name="mean", bufs=1))
 
-        rows = keep.tile([P, 3, D], BF16)
-        nc.vector.memset(rows[:].bitcast(I32), 0)
         w_planes = keep.tile([P, 2, PASSES, D], U8, align_bytes=64)
         nc.vector.memset(w_planes[:].bitcast(I32), 0)
+        rows = keep.tile([P, 3, D], BF16)
+        nc.vector.memset(rows[:].bitcast(I32), 0)
         ones = keep.tile([P, P], BF16)
         nc.vector.memset(ones[:], 1.0)
         eps = keep.tile([P, 1], F32)
         nc.vector.memset(eps[:], LN_EPS)
-        ident_bf16 = keep.tile([P, P], BF16)
-        make_identity(nc, ident_bf16[:])
         ident_f32 = keep.tile([P, P], F32)
         make_identity(nc, ident_f32[:])
         warm = keep.tile([P, 1], F32)
         nc.scalar.activation(out=warm[:], in_=eps[:], func=ACT.Abs_reciprocal_sqrt)
 
-        h_loads = []
-        for first in range(0, NODES, LOAD_NODES):
-            count = min(LOAD_NODES, NODES - first)
-            h_load = keep.tile([P, count, D], BF16, name="h_load%d" % first)
-            nc.sync.dma_start(out=h_load[:], in_=h[:, first : first + count, :])
-            h_loads.append(h_load)
-            if first == 0:
-                for j, vec in enumerate((b_l, ln_g, ln_b)):
-                    nc.sync.dma_start(out=rows[0:1, j, :], in_=vec.unsqueeze(0))
-        for w, (words, scales) in enumerate(weights):
-            for quad in range(4):
-                nc.sync.dma_start(
-                    out=w_planes[32 * quad : 32 * quad + 4, w, :, :].bitcast(I32),
-                    in_=scales[:, 4 * quad : 4 * quad + 4, :].rearrange("g r n -> r g n").bitcast(I32),
-                )
+        def make_neighbours(first, columns):
+            graphs = columns // NODES
+            near = keep.tile([P, columns], BF16, name="near%d" % first)
+            nc.gpsimd.memset(near[:], 1.0 / (NODES - 1))
+            nc.gpsimd.affine_select(
+                out=near[:], in_=near[:], compare_op=ALU.is_ge, fill=0.0,
+                base=-first, pattern=[[-NODES, graphs], [0, NODES]], channel_multiplier=1,
+            )
+            nc.gpsimd.affine_select(
+                out=near[:], in_=near[:], compare_op=ALU.is_ge, fill=0.0,
+                base=first + NODES - 1, pattern=[[NODES, graphs], [0, NODES]], channel_multiplier=-1,
+            )
+            nc.gpsimd.affine_select(
+                out=near[:], in_=near[:], compare_op=ALU.not_equal, fill=0.0,
+                base=-first, pattern=[[-1, columns]], channel_multiplier=1,
+            )
+            return near
+
+        last_columns = ROWS - (GROUPS - 1) * GROUP
+        near_first = make_neighbours(0, GROUP)
+        near_last = make_neighbours(P - last_columns, last_columns)
+
+        windows = {}
+        tiles = {}
+
+        def load_rows(kind, index, first):
+            loaded = keep.tile([P, D], BF16, name="%s%d" % (kind, index))
+            nc.sync.dma_start(out=loaded[:], in_=h_rows[first : first + P, :])
+            return loaded
+
+        def load_window(a):
+            windows[a] = load_rows("window", a, min(a * GROUP, LAST_WINDOW))
+
         w_words = keep.tile([P, 2, PASSES, D], U32, align_bytes=64)
-        for w, (words, scales) in enumerate(weights):
+
+        def load_scales():
+            for w, (words, scales) in enumerate(weights):
+                for quad in range(4):
+                    nc.sync.dma_start(
+                        out=w_planes[32 * quad : 32 * quad + 4, w, :, :].bitcast(I32),
+                        in_=scales[:, 4 * quad : 4 * quad + 4, :].rearrange("g r n -> r g n").bitcast(I32),
+                    )
+
+        def load_words(w):
             for g in range(PASSES):
                 nc.sync.dma_start(
                     out=w_words[:, w, g, :].bitcast(I32),
-                    in_=words[g].rearrange("p n t -> p (n t)").bitcast(I32),
+                    in_=weights[w][0][g].rearrange("p n t -> p (n t)").bitcast(I32),
                 )
 
-        def h_node(i):
-            return h_loads[i // LOAD_NODES][:, i % LOAD_NODES, :]
+        def load_all():
+            load_window(0)
+            tiles[0] = windows[0]
+            load_window(1)
+            for j, vec in enumerate((b_l, ln_g, ln_b)):
+                nc.sync.dma_start(out=rows[0:1, j, :], in_=vec.unsqueeze(0))
+            load_scales()
+            load_words(0)
+            for i in range(1, TILES):
+                tiles[i] = load_rows("tile", i, i * P)
+                load_window(i + 1)
+                if i == 1:
+                    load_words(1)
+            load_window(GROUPS - 1)
 
-        flipped = {}
         x_ts = {}
         sides_of = {}
         product = {}
@@ -97,46 +137,56 @@ def tile_gnnnicheencoder_pa_kernel(
         halves = [slice(half * N_TILE, (half + 1) * N_TILE) for half in range(HALVES)]
         whole = slice(0, D)
 
-        def transpose_h(j):
-            pairs = h_node(j).bitcast(F32)
-            early = j < EARLY_NODES
-            flipped[j] = flip.tile([P, PASSES, 2, P] if early else [P, PASSES, P, 2], F32, tag="flip", name="flipped")
+        def operands_of(j):
+            if j not in x_ts:
+                x_ts[j] = swap.tile([P, 2, D], BF16, align_bytes=64, name="x_t")
+            return x_ts[j]
+
+        def transpose_h(j, pool, tag):
+            pairs = tiles[j][:].bitcast(F32)
+            flipped = pool.tile([P, PASSES, 2, P], F32, tag=tag, name="flipped")
             for g in range(PASSES):
                 for u in range(2):
                     nc.tensor.transpose(
-                        out=flipped[j][:, g, u, :] if early else flipped[j][:, g, :, u],
-                        in_=pairs[:, 256 * g + u : 256 * (g + 1) : 2],
-                        identity=ident_f32[:],
+                        out=flipped[:, g, u, :], in_=pairs[:, 256 * g + u : 256 * (g + 1) : 2], identity=ident_f32[:]
                     )
-            x_ts[j] = swap.tile([P, 2, D], BF16, tag="swap", align_bytes=64, name="x_t")
-            if early:
-                nc.scalar.copy(
-                    out=x_ts[j][:, 0, :].bitcast(F32).rearrange("p (g b u) -> p g b u", g=PASSES, u=2),
-                    in_=flipped[j][:].rearrange("p g u b -> p g b u"),
-                )
-            else:
-                nc.scalar.copy(out=x_ts[j][:, 0, :].bitcast(F32), in_=flipped[j][:].rearrange("p g b u -> p (g b u)"))
-
-        def mean_of_neighbours(j, g):
-            cols = slice(g * K_PASS, (g + 1) * K_PASS)
-            if j < EARLY_NODES:
-                nc.vector.scalar_tensor_tensor(
-                    out=x_ts[j][:, 1, cols].rearrange("p (b t) -> p b t", t=PACK),
-                    in0=x_ts[j][:, 0, cols].rearrange("p (b t) -> p b t", t=PACK),
-                    scalar=-1.0 / (NODES - 1),
-                    in1=total_ps[g][:].rearrange("p t b -> p b t"),
-                    op0=ALU.mult,
-                    op1=ALU.add,
-                )
-                return
-            nc.vector.scalar_tensor_tensor(
-                out=x_ts[j][:, 1, cols],
-                in0=flipped[j][:, g].rearrange("p b u -> p (b u)").bitcast(BF16),
-                scalar=-1.0 / (NODES - 1),
-                in1=total_t[:, cols],
-                op0=ALU.mult,
-                op1=ALU.add,
+            nc.scalar.copy(
+                out=operands_of(j)[:, 0, :].bitcast(F32).rearrange("p (g b u) -> p g b u", g=PASSES, u=2),
+                in_=flipped[:].rearrange("p g u b -> p g b u"),
             )
+
+        def mean_of_neighbours(a, pool, tag, copy_out):
+            near = near_first if a < GROUPS - 1 else near_last
+            columns = min(GROUP, ROWS - a * GROUP)
+            mean_ps = pool.tile([P, PASSES, PACK, MEAN_PITCH], BF16, tag=tag, name="mean_ps")
+            for g in range(PASSES):
+                for t in range(PACK):
+                    nc.tensor.matmul(
+                        out=mean_ps[:, g, t, :columns],
+                        lhsT=windows[a][:, g * K_PASS + t : (g + 1) * K_PASS : PACK],
+                        rhs=near[:],
+                        start=True,
+                        stop=True,
+                    )
+            first = a * GROUP
+            while first < a * GROUP + columns:
+                j = first // P
+                end = min((j + 1) * P, a * GROUP + columns)
+                copy_out(
+                    out=operands_of(j)[:, 1, :].rearrange("p (g b t) -> p g b t", g=PASSES, t=PACK)[
+                        :, :, first - j * P : end - j * P, :
+                    ],
+                    in_=mean_ps[:, :, :, first - a * GROUP : end - a * GROUP].rearrange("p g t b -> p g b t"),
+                )
+                first = end
+
+        groups_done = []
+
+        def prepare(j):
+            transpose_h(j, flip, "flip")
+            while len(groups_done) * GROUP < min((j + 1) * P, ROWS):
+                mean_of_neighbours(len(groups_done), mean, "mean", nc.scalar.copy)
+                groups_done.append(j)
 
         def quantise(j):
             codes = sides.tile([P, 2 * PASSES * P], U32, align_bytes=64)
@@ -146,25 +196,28 @@ def tile_gnnnicheencoder_pa_kernel(
             )
             sides_of[j] = (codes, plane)
 
-        def multiply(j):
+        def multiply_part(j, w, half):
             codes, plane = sides_of[j]
-            product[j] = []
+            for g in range(PASSES):
+                columns = slice((w * PASSES + g) * P, (w * PASSES + g + 1) * P)
+                nc.tensor.matmul_mx(
+                    out=product[j][half][:],
+                    lhsT=codes[:, columns].bitcast(FP8X4),
+                    lhsT_scale=plane[:, columns],
+                    rhs=w_words[:, w, g, halves[half]].bitcast(FP8X4),
+                    rhs_scale=w_planes[:, w, g, halves[half]],
+                    start=(w == 0 and g == 0),
+                    stop=(w == 1 and g == PASSES - 1),
+                )
+
+        def open_product(j):
+            product[j] = [prod.tile([P, N_TILE], F32, tag="prod", name="acc") for half in range(HALVES)]
+
+        def multiply(j):
+            open_product(j)
             for half in range(HALVES):
-                cols = slice(half * N_TILE, (half + 1) * N_TILE)
-                acc = prod.tile([P, N_TILE], F32, tag="prod")
                 for w in range(2):
-                    for g in range(PASSES):
-                        graphs = slice((w * PASSES + g) * P, (w * PASSES + g + 1) * P)
-                        nc.tensor.matmul_mx(
-                            out=acc[:],
-                            lhsT=codes[:, graphs].bitcast(FP8X4),
-                            lhsT_scale=plane[:, graphs],
-                            rhs=w_words[:, w, g, cols].bitcast(FP8X4),
-                            rhs_scale=w_planes[:, w, g, cols],
-                            start=(w == 0 and g == 0),
-                            stop=(w == 1 and g == PASSES - 1),
-                        )
-                product[j].append(acc)
+                    multiply_part(j, w, half)
 
         def spread_over_partitions(j, spread):
             for half in range(HALVES):
@@ -223,21 +276,17 @@ def tile_gnnnicheencoder_pa_kernel(
                 out=lifts[i][:, cols], in_=ys[i][:, cols], func=ACT.Relu, scale=-(1.0 - LEAKY_SLOPE)
             )
 
-        def finish_on_gpsimd(i, cols):
-            y_plus_h = swap.tile([P, D], F32, tag="swap", align_bytes=64)
-            nc.gpsimd.tensor_tensor(out=y_plus_h[:, cols], in0=ys[i][:, cols], in1=h_node(i)[:, cols], op=ALU.add)
-            result = work.tile([P, D], F32)
-            nc.gpsimd.tensor_tensor(out=result[:, cols], in0=y_plus_h[:, cols], in1=lifts[i][:, cols], op=ALU.add)
-            nc.sync.dma_start(out=out[:, i, cols], in_=result[:, cols])
+        def store(i, cols, result):
+            nc.sync.dma_start(out=out_rows[i * P : (i + 1) * P, cols], in_=result)
 
-        def finish_in_halves_on_gpsimd(i):
-            y_plus_h = swap.tile([P, D], F32, tag="swap", align_bytes=64)
-            for cols in halves:
-                nc.gpsimd.tensor_tensor(out=y_plus_h[:, cols], in0=ys[i][:, cols], in1=h_node(i)[:, cols], op=ALU.add)
+        def finish_on_gpsimd(i, parts):
+            y_plus_h = work.tile([P, D], F32)
+            for cols in parts:
+                nc.gpsimd.tensor_tensor(out=y_plus_h[:, cols], in0=ys[i][:, cols], in1=tiles[i][:, cols], op=ALU.add)
             result = work.tile([P, D], F32)
-            for cols in halves:
+            for cols in parts:
                 nc.gpsimd.tensor_tensor(out=result[:, cols], in0=y_plus_h[:, cols], in1=lifts[i][:, cols], op=ALU.add)
-                nc.sync.dma_start(out=out[:, i, cols], in_=result[:, cols])
+                store(i, cols, result[:, cols])
 
         def leaky_on_vector(i, cols):
             leaky = work.tile([P, N_TILE], F32)
@@ -248,75 +297,60 @@ def tile_gnnnicheencoder_pa_kernel(
 
         def add_h_on_vector(i, cols, leaky):
             result_v = work.tile([P, N_TILE], F32)
-            nc.vector.tensor_tensor(out=result_v[:], in0=leaky[:], in1=h_node(i)[:, cols], op=ALU.add)
-            nc.sync.dma_start(out=out[:, i, cols], in_=result_v[:])
+            nc.vector.tensor_tensor(out=result_v[:], in0=leaky[:], in1=tiles[i][:, cols], op=ALU.add)
+            store(i, cols, result_v[:])
 
-        total = [prod.tile([P, K_PASS], F32, tag="prod", name="total%d" % g) for g in range(PASSES)]
-        for i in range(NODES):
-            for g in range(PASSES):
-                nc.tensor.matmul(
-                    out=total[g][:],
-                    lhsT=ident_bf16[:],
-                    rhs=h_node(i)[:, g * K_PASS : (g + 1) * K_PASS],
-                    start=(i == 0),
-                    stop=(i == NODES - 1),
-                )
-        transpose_h(0)
-        transpose_h(1)
-        total_sb = keep.tile([P, PASSES, PACK, P], F32)
-        scaled_copy = (nc.scalar.mul, nc.vector.tensor_scalar_mul)
-        for g in range(PASSES):
-            scaled_copy[g](total_sb[:, g], total[g][:].rearrange("b (p t) -> b t p", t=PACK), 1.0 / (NODES - 1))
-        total_ps = [psum_keep.tile([P, PACK, P], F32, tag=LATER_IN_BANK[g], name="total_ps%d" % g) for g in range(PASSES)]
-        for g in range(PASSES):
-            for t in range(PACK):
-                nc.tensor.transpose(out=total_ps[g][:, t, :], in_=total_sb[:, g, t, :], identity=ident_f32[:])
-        for g in range(PASSES):
-            mean_of_neighbours(0, g)
-        total_t = keep.tile([P, D], F32)
-        for g in range(PASSES):
-            nc.scalar.copy(
-                out=total_t[:, g * K_PASS : (g + 1) * K_PASS].rearrange("p (b t) -> p b t", t=PACK),
-                in_=total_ps[g][:].rearrange("p t b -> p b t"),
-            )
-        bias_ps = prod.tile([P, D], BF16, tag="prod")
-        spread_over_partitions(0, bias_ps)
-        bias_sb = keep.tile([P, D], BF16)
-        nc.scalar.copy(out=bias_sb[:], in_=bias_ps[:])
+        LAST = TILES - 1
 
-        LAST = NODES - 1
-
-        with tc.manual_schedule(engines={mybir.EngineType.DVE}):
-            for i in range(-AHEAD_QUANTISE, LAST):
-                if 0 <= i + AHEAD_QUANTISE:
-                    quantise(i + AHEAD_QUANTISE)
-                    multiply(i + AHEAD_QUANTISE)
-                if i >= 1:
-                    finish_on_gpsimd(i - 1, whole)
-                if i >= 0:
-                    add_bias(i, 0)
-                    add_bias(i, 1)
-                    statistics(i)
-                if 2 <= i + AHEAD_TRANSPOSE < NODES:
-                    transpose_h(i + AHEAD_TRANSPOSE)
-                for step in range(2):
-                    if i + AHEAD_MEAN < NODES:
-                        mean_of_neighbours(i + AHEAD_MEAN, step)
-                    elif i == LAST - 1:
-                        add_bias(LAST, step)
-                    if step == 0 and i >= 0:
-                        centre_and_gain(i, whole)
-                if i + AHEAD_MEAN == EARLY_NODES - 1:
-                    gain_ps = psum_keep.tile([P, D], BF16, tag=LATER_IN_BANK[0])
-                    spread_over_partitions(1, gain_ps)
-                    shift_ps = psum_keep.tile([P, D], BF16, tag=LATER_IN_BANK[1])
-                    spread_over_partitions(2, shift_ps)
-                if i == LAST - 1:
-                    statistics(LAST)
-                if i >= 0:
-                    scale_and_shift(i, whole)
-                    lift_negatives(i, whole)
-            finish_in_halves_on_gpsimd(LAST - 1)
+        ordered = {
+            mybir.EngineType.DVE, mybir.EngineType.PE, mybir.EngineType.Activation, mybir.EngineType.SP
+        }
+        with tc.manual_schedule(engines=ordered):
+            load_all()
+            transpose_h(0, flip, "flip")
+            mean_of_neighbours(0, mean, "mean", nc.vector.tensor_copy)
+            mean_of_neighbours(1, prod, "prod", nc.vector.tensor_copy)
+            quantise(0)
+            bias_ps = prod.tile([P, D], BF16, tag="prod")
+            spread_over_partitions(0, bias_ps)
+            bias_sb = keep.tile([P, D], BF16)
+            nc.scalar.copy(out=bias_sb[:], in_=bias_ps[:])
+            gain_ps = psum_keep.tile([P, D], BF16)
+            spread_over_partitions(1, gain_ps)
+            shift_ps = psum_keep.tile([P, D], BF16)
+            spread_over_partitions(2, shift_ps)
+            open_product(0)
+            for half in range(HALVES):
+                multiply_part(0, 0, half)
+            transpose_h(1, flip, "flip")
+            mean_of_neighbours(2, mean, "mean", nc.scalar.copy)
+            groups_done.extend([0, 1, 2])
+            for half in range(HALVES):
+                multiply_part(0, 1, half)
+            quantise(1)
+            prepare(2)
+            multiply(1)
+            add_bias(0, 0)
+            add_bias(0, 1)
+            statistics(0)
+            for i in range(LAST):
+                if i + 2 < TILES:
+                    quantise(i + 2)
+                    if i + 3 < TILES:
+                        prepare(i + 3)
+                    multiply(i + 2)
+                if i == 0:
+                    centre_and_gain(i, whole)
+                    add_bias(i + 1, 0)
+                else:
+                    finish_on_gpsimd(i - 1, [whole])
+                    add_bias(i + 1, 0)
+                    centre_and_gain(i, whole)
+                add_bias(i + 1, 1)
+                statistics(i + 1)
+                scale_and_shift(i, whole)
+                lift_negatives(i, whole)
+            finish_on_gpsimd(LAST - 1, halves)
             for cols in halves:
                 centre_and_gain(LAST, cols)
             for cols in halves:

@@ -28,6 +28,7 @@ LEAKY_SLOPE = 0.01
 GROUP = (P // NODES) * NODES
 GROUPS = -(-ROWS // GROUP)
 LAST_WINDOW = ROWS - P
+SHARED = 320
 MEAN_PITCH = 120
 
 FLOPS = 2 * 2 * ROWS * D * D
@@ -48,7 +49,7 @@ def tile_gnnnicheencoder_pa_kernel(
         work = stack.enter_context(tc.tile_pool(name="work", bufs=3))
         small = stack.enter_context(tc.tile_pool(name="small", bufs=4))
         psum_keep = stack.enter_context(tc.psum_pool(name="psum_keep", bufs=1))
-        prod = stack.enter_context(tc.psum_pool(name="prod", bufs=4))
+        prod = stack.enter_context(tc.psum_pool(name="prod", bufs=3))
         flip = stack.enter_context(tc.psum_pool(name="flip", bufs=1))
         mean = stack.enter_context(tc.psum_pool(name="mean", bufs=1))
 
@@ -62,6 +63,8 @@ def tile_gnnnicheencoder_pa_kernel(
         nc.vector.memset(eps[:], LN_EPS)
         ident_f32 = keep.tile([P, P], F32)
         make_identity(nc, ident_f32[:])
+        ident_bf16 = keep.tile([P, P], BF16)
+        nc.vector.tensor_copy(out=ident_bf16[:], in_=ident_f32[:])
         warm = keep.tile([P, 1], F32)
         nc.scalar.activation(out=warm[:], in_=eps[:], func=ACT.Abs_reciprocal_sqrt)
 
@@ -136,6 +139,9 @@ def tile_gnnnicheencoder_pa_kernel(
         cs, sums_of, neg_means, rstds, centreds, ys, lifts = {}, {}, {}, {}, {}, {}, {}
         halves = [slice(half * N_TILE, (half + 1) * N_TILE) for half in range(HALVES)]
         whole = slice(0, D)
+        gpsimd_part = slice(0, D - SHARED)
+        vector_part = slice(D - SHARED, D)
+        h_sums, y_plus_hs = {}, {}
 
         def operands_of(j):
             if j not in x_ts:
@@ -182,11 +188,17 @@ def tile_gnnnicheencoder_pa_kernel(
 
         groups_done = []
 
+        def groups_wanted(j):
+            return -(-min((j + 1) * P, ROWS) // GROUP)
+
+        def next_group():
+            mean_of_neighbours(len(groups_done), mean, "mean", nc.scalar.copy)
+            groups_done.append(len(groups_done))
+
         def prepare(j):
             transpose_h(j, flip, "flip")
-            while len(groups_done) * GROUP < min((j + 1) * P, ROWS):
-                mean_of_neighbours(len(groups_done), mean, "mean", nc.scalar.copy)
-                groups_done.append(j)
+            while len(groups_done) < groups_wanted(j):
+                next_group()
 
         def quantise(j):
             codes = sides.tile([P, 2 * PASSES * P], U32, align_bytes=64)
@@ -211,13 +223,12 @@ def tile_gnnnicheencoder_pa_kernel(
                 )
 
         def open_product(j):
-            product[j] = [prod.tile([P, N_TILE], F32, tag="prod", name="acc") for half in range(HALVES)]
+            product.setdefault(j, []).append(prod.tile([P, N_TILE], F32, tag="prod", name="acc"))
 
-        def multiply(j):
+        def multiply(j, half):
             open_product(j)
-            for half in range(HALVES):
-                for w in range(2):
-                    multiply_part(j, w, half)
+            for w in range(2):
+                multiply_part(j, w, half)
 
         def spread_over_partitions(j, spread):
             for half in range(HALVES):
@@ -279,10 +290,21 @@ def tile_gnnnicheencoder_pa_kernel(
         def store(i, cols, result):
             nc.sync.dma_start(out=out_rows[i * P : (i + 1) * P, cols], in_=result)
 
+        def spread_h(i):
+            h_sums[i] = psum_keep.tile([P, SHARED], F32, name="h_ps")
+            nc.tensor.matmul(out=h_sums[i][:], lhsT=ident_bf16[:], rhs=tiles[i][:, vector_part], start=True, stop=True)
+
+        def add_h_for_gpsimd(i):
+            y_plus_hs[i] = work.tile([P, D], F32, name="y_plus_h")
+            nc.vector.tensor_tensor(
+                out=y_plus_hs[i][:, vector_part], in0=ys[i][:, vector_part], in1=h_sums[i][:], op=ALU.add
+            )
+
         def finish_on_gpsimd(i, parts):
-            y_plus_h = work.tile([P, D], F32)
-            for cols in parts:
-                nc.gpsimd.tensor_tensor(out=y_plus_h[:, cols], in0=ys[i][:, cols], in1=tiles[i][:, cols], op=ALU.add)
+            y_plus_h = y_plus_hs[i]
+            nc.gpsimd.tensor_tensor(
+                out=y_plus_h[:, gpsimd_part], in0=ys[i][:, gpsimd_part], in1=tiles[i][:, gpsimd_part], op=ALU.add
+            )
             result = work.tile([P, D], F32)
             for cols in parts:
                 nc.gpsimd.tensor_tensor(out=result[:, cols], in0=y_plus_h[:, cols], in1=lifts[i][:, cols], op=ALU.add)
@@ -319,8 +341,8 @@ def tile_gnnnicheencoder_pa_kernel(
             spread_over_partitions(1, gain_ps)
             shift_ps = psum_keep.tile([P, D], BF16)
             spread_over_partitions(2, shift_ps)
-            open_product(0)
             for half in range(HALVES):
+                open_product(0)
                 multiply_part(0, 0, half)
             transpose_h(1, flip, "flip")
             mean_of_neighbours(2, mean, "mean", nc.scalar.copy)
@@ -329,8 +351,9 @@ def tile_gnnnicheencoder_pa_kernel(
                 multiply_part(0, 1, half)
             quantise(1)
             prepare(2)
-            multiply(1)
+            multiply(1, 0)
             add_bias(0, 0)
+            multiply(1, 1)
             add_bias(0, 1)
             statistics(0)
             for i in range(LAST):
@@ -338,7 +361,11 @@ def tile_gnnnicheencoder_pa_kernel(
                     quantise(i + 2)
                     if i + 3 < TILES:
                         prepare(i + 3)
-                    multiply(i + 2)
+                if i >= 1:
+                    add_h_for_gpsimd(i - 1)
+                spread_h(i)
+                if i + 2 < TILES:
+                    multiply(i + 2, 0)
                 if i == 0:
                     centre_and_gain(i, whole)
                     add_bias(i + 1, 0)
@@ -346,10 +373,15 @@ def tile_gnnnicheencoder_pa_kernel(
                     finish_on_gpsimd(i - 1, [whole])
                     add_bias(i + 1, 0)
                     centre_and_gain(i, whole)
+                if i + 2 < TILES:
+                    multiply(i + 2, 1)
                 add_bias(i + 1, 1)
                 statistics(i + 1)
+                if i + 4 < TILES and groups_wanted(i + 4) > len(groups_done) + 1:
+                    next_group()
                 scale_and_shift(i, whole)
                 lift_negatives(i, whole)
+            add_h_for_gpsimd(LAST - 1)
             finish_on_gpsimd(LAST - 1, halves)
             for cols in halves:
                 centre_and_gain(LAST, cols)

@@ -28,7 +28,7 @@ LEAKY_SLOPE = 0.01
 GROUP = (P // NODES) * NODES
 GROUPS = -(-ROWS // GROUP)
 LAST_WINDOW = ROWS - P
-SHARED = 320
+SHARED = 432
 MEAN_PITCH = 120
 
 FLOPS = 2 * 2 * ROWS * D * D

@@ -28,7 +28,7 @@ LEAKY_SLOPE = 0.01
 GROUP = (P // NODES) * NODES
 GROUPS = -(-ROWS // GROUP)
 LAST_WINDOW = ROWS - P
-SHARED = 432
+SHARED = 384
 MEAN_PITCH = 120
 
 FLOPS = 2 * 2 * ROWS * D * D
@@ -282,7 +282,8 @@ def tile_gnnnicheencoder_pa_kernel(
             )
 
         def lift_negatives(i, cols):
-            lifts[i] = work.tile([P, D], F32, name="lift")
+            if cols.start == 0:
+                lifts[i] = work.tile([P, D], F32, name="lift")
             nc.scalar.activation(
                 out=lifts[i][:, cols], in_=ys[i][:, cols], func=ACT.Relu, scale=-(1.0 - LEAKY_SLOPE)
             )
@@ -310,17 +311,32 @@ def tile_gnnnicheencoder_pa_kernel(
                 nc.gpsimd.tensor_tensor(out=result[:, cols], in0=y_plus_h[:, cols], in1=lifts[i][:, cols], op=ALU.add)
                 store(i, cols, result[:, cols])
 
-        def leaky_on_vector(i, cols):
-            leaky = work.tile([P, N_TILE], F32)
-            nc.vector.scalar_tensor_tensor(
-                out=leaky[:], in0=ys[i][:, cols], scalar=LEAKY_SLOPE, in1=ys[i][:, cols], op0=ALU.mult, op1=ALU.max
-            )
-            return leaky
+        def transpose_back(i):
+            back = mean.tile([P, PASSES, PACK, P], BF16, tag="mean", name="back")
+            for g in range(PASSES):
+                for t in range(PACK):
+                    nc.tensor.transpose(
+                        out=back[:, g, t, :],
+                        in_=x_ts[i][:, 0, g * K_PASS + t : (g + 1) * K_PASS : PACK],
+                        identity=ident_bf16[:],
+                    )
+            return back
 
-        def add_h_on_vector(i, cols, leaky):
-            result_v = work.tile([P, N_TILE], F32)
-            nc.vector.tensor_tensor(out=result_v[:], in0=leaky[:], in1=tiles[i][:, cols], op=ALU.add)
-            store(i, cols, result_v[:])
+        def finish_on_vector(i):
+            y_plus_h = work.tile([P, D], F32, name="y_plus_h")
+            for g, cols in enumerate(halves):
+                nc.vector.tensor_tensor(
+                    out=y_plus_h[:, cols].rearrange("r (p t) -> r p t", t=PACK),
+                    in0=ys[i][:, cols].rearrange("r (p t) -> r p t", t=PACK),
+                    in1=back[:, g].rearrange("r t p -> r p t"),
+                    op=ALU.add,
+                )
+            result_v = work.tile([P, D], F32, name="result")
+            for cols in halves:
+                nc.vector.tensor_tensor(
+                    out=result_v[:, cols], in0=y_plus_h[:, cols], in1=lifts[i][:, cols], op=ALU.add
+                )
+                store(i, cols, result_v[:, cols])
 
         LAST = TILES - 1
 
@@ -381,12 +397,12 @@ def tile_gnnnicheencoder_pa_kernel(
                     next_group()
                 scale_and_shift(i, whole)
                 lift_negatives(i, whole)
+            back = transpose_back(LAST)
             add_h_for_gpsimd(LAST - 1)
             finish_on_gpsimd(LAST - 1, halves)
             for cols in halves:
                 centre_and_gain(LAST, cols)
             for cols in halves:
                 scale_and_shift(LAST, cols)
-            leaky_last = [leaky_on_vector(LAST, cols) for cols in halves]
-            for cols, leaky in zip(halves, leaky_last):
-                add_h_on_vector(LAST, cols, leaky)
+                lift_negatives(LAST, cols)
+            finish_on_vector(LAST)

@@ -29,6 +29,7 @@ GROUP = (P // NODES) * NODES
 GROUPS = -(-ROWS // GROUP)
 LAST_WINDOW = ROWS - P
 SHARED = 384
+LAST_STORE = 128
 MEAN_PITCH = 120
 
 FLOPS = 2 * 2 * ROWS * D * D
@@ -123,14 +124,15 @@ def tile_gnnnicheencoder_pa_kernel(
             tiles[0] = windows[0]
             load_window(1)
             for j, vec in enumerate((b_l, ln_g, ln_b)):
-                nc.sync.dma_start(out=rows[0:1, j, :], in_=vec.unsqueeze(0))
+                nc.scalar.dma_start(out=rows[0:1, j, :], in_=vec.unsqueeze(0))
             load_scales()
             load_words(0)
+            load_window(2)
+            load_words(1)
             for i in range(1, TILES):
                 tiles[i] = load_rows("tile", i, i * P)
-                load_window(i + 1)
-                if i == 1:
-                    load_words(1)
+                if i > 1:
+                    load_window(i + 1)
             load_window(GROUPS - 1)
 
         x_ts = {}
@@ -145,60 +147,62 @@ def tile_gnnnicheencoder_pa_kernel(
 
         def operands_of(j):
             if j not in x_ts:
-                x_ts[j] = swap.tile([P, 2, D], BF16, align_bytes=64, name="x_t")
+                x_ts[j] = swap.tile([P, 2, D], BF16, tag="swap", align_bytes=64, name="x_t")
             return x_ts[j]
 
-        def transpose_h(j, pool, tag):
-            pairs = tiles[j][:].bitcast(F32)
-            flipped = pool.tile([P, PASSES, 2, P], F32, tag=tag, name="flipped")
+        def transpose_rows(source):
+            pairs = source[:].bitcast(F32)
+            flipped = flip.tile([P, PASSES, 2, P], F32)
             for g in range(PASSES):
                 for u in range(2):
                     nc.tensor.transpose(
                         out=flipped[:, g, u, :], in_=pairs[:, 256 * g + u : 256 * (g + 1) : 2], identity=ident_f32[:]
                     )
+            return flipped
+
+        def copy_h(j, flipped, columns=slice(0, P), first=0):
             nc.scalar.copy(
-                out=operands_of(j)[:, 0, :].bitcast(F32).rearrange("p (g b u) -> p g b u", g=PASSES, u=2),
-                in_=flipped[:].rearrange("p g u b -> p g b u"),
+                out=operands_of(j)[:, 0, :].bitcast(F32).rearrange("p (g b u) -> p g b u", g=PASSES, u=2)[:, :, columns, :],
+                in_=flipped[:, :, :, first : first + columns.stop - columns.start].rearrange("p g u b -> p g b u"),
             )
 
-        def mean_of_neighbours(a, pool, tag, copy_out):
+        means = []
+
+        def columns_of(a):
+            return min(GROUP, ROWS - a * GROUP)
+
+        def groups_wanted(j):
+            return -(-min((j + 1) * P, ROWS) // GROUP)
+
+        def next_group(pool, tag):
+            a = len(means)
             near = near_first if a < GROUPS - 1 else near_last
-            columns = min(GROUP, ROWS - a * GROUP)
             mean_ps = pool.tile([P, PASSES, PACK, MEAN_PITCH], BF16, tag=tag, name="mean_ps")
             for g in range(PASSES):
                 for t in range(PACK):
                     nc.tensor.matmul(
-                        out=mean_ps[:, g, t, :columns],
+                        out=mean_ps[:, g, t, : columns_of(a)],
                         lhsT=windows[a][:, g * K_PASS + t : (g + 1) * K_PASS : PACK],
                         rhs=near[:],
                         start=True,
                         stop=True,
                     )
-            first = a * GROUP
-            while first < a * GROUP + columns:
-                j = first // P
-                end = min((j + 1) * P, a * GROUP + columns)
-                copy_out(
-                    out=operands_of(j)[:, 1, :].rearrange("p (g b t) -> p g b t", g=PASSES, t=PACK)[
-                        :, :, first - j * P : end - j * P, :
-                    ],
-                    in_=mean_ps[:, :, :, first - a * GROUP : end - a * GROUP].rearrange("p g t b -> p g b t"),
-                )
-                first = end
+            means.append(mean_ps)
 
-        groups_done = []
+        def copy_mean(a, j, copy_out):
+            first = max(a * GROUP, j * P)
+            end = min(a * GROUP + columns_of(a), (j + 1) * P)
+            copy_out(
+                out=operands_of(j)[:, 1, :].rearrange("p (g b t) -> p g b t", g=PASSES, t=PACK)[
+                    :, :, first - j * P : end - j * P, :
+                ],
+                in_=means[a][:, :, :, first - a * GROUP : end - a * GROUP].rearrange("p g t b -> p g b t"),
+            )
 
-        def groups_wanted(j):
-            return -(-min((j + 1) * P, ROWS) // GROUP)
-
-        def next_group():
-            mean_of_neighbours(len(groups_done), mean, "mean", nc.scalar.copy)
-            groups_done.append(len(groups_done))
-
-        def prepare(j):
-            transpose_h(j, flip, "flip")
-            while len(groups_done) < groups_wanted(j):
-                next_group()
+        def copy_last_group():
+            a = len(means) - 1
+            for j in range(a * GROUP // P, (a * GROUP + columns_of(a) - 1) // P + 1):
+                copy_mean(a, j, nc.scalar.copy)
 
         def quantise(j):
             codes = sides.tile([P, 2 * PASSES * P], U32, align_bytes=64)
@@ -249,12 +253,14 @@ def tile_gnnnicheencoder_pa_kernel(
                 accum_out=sums_of[i][:, half : half + 1],
             )
 
-        def statistics(i):
+        def negative_mean(i):
             neg_means[i] = small.tile([P, 1], F32, name="neg_mean")
             scaled_sums = small.tile([P, HALVES], F32)
             nc.scalar.activation(
                 out=scaled_sums[:], in_=sums_of[i][:], func=ACT.Copy, scale=-1.0 / D, accum_out=neg_means[i][:]
             )
+
+        def deviation(i):
             squares = work.tile([P, D], BF16)
             sum_sq = small.tile([P, 1], F32)
             nc.scalar.activation(
@@ -332,7 +338,7 @@ def tile_gnnnicheencoder_pa_kernel(
                     op=ALU.add,
                 )
             result_v = work.tile([P, D], F32, name="result")
-            for cols in halves:
+            for cols in (halves[0], slice(N_TILE, D - LAST_STORE), slice(D - LAST_STORE, D)):
                 nc.vector.tensor_tensor(
                     out=result_v[:, cols], in0=y_plus_h[:, cols], in1=lifts[i][:, cols], op=ALU.add
                 )
@@ -345,10 +351,15 @@ def tile_gnnnicheencoder_pa_kernel(
         }
         with tc.manual_schedule(engines=ordered):
             load_all()
-            transpose_h(0, flip, "flip")
-            mean_of_neighbours(0, mean, "mean", nc.vector.tensor_copy)
-            mean_of_neighbours(1, prod, "prod", nc.vector.tensor_copy)
+            on_vector, on_scalar = nc.vector.tensor_copy, nc.scalar.copy
+            copy_h(0, transpose_rows(windows[0]))
+            next_group(mean, "mean")
+            copy_mean(0, 0, on_vector)
+            next_group(prod, "prod")
+            copy_mean(1, 0, on_vector)
+            copy_mean(1, 1, on_vector)
             quantise(0)
+            copy_h(1, transpose_rows(windows[1]), slice(0, GROUP), P - GROUP)
             bias_ps = prod.tile([P, D], BF16, tag="prod")
             spread_over_partitions(0, bias_ps)
             bias_sb = keep.tile([P, D], BF16)
@@ -360,41 +371,48 @@ def tile_gnnnicheencoder_pa_kernel(
             for half in range(HALVES):
                 open_product(0)
                 multiply_part(0, 0, half)
-            transpose_h(1, flip, "flip")
-            mean_of_neighbours(2, mean, "mean", nc.scalar.copy)
-            groups_done.extend([0, 1, 2])
+            copy_h(1, transpose_rows(windows[2]), slice(GROUP, P), P - GROUP)
+            next_group(mean, "mean")
+            copy_last_group()
             for half in range(HALVES):
                 multiply_part(0, 1, half)
             quantise(1)
-            prepare(2)
+            flipped = transpose_rows(tiles[2])
+            next_group(mean, "mean")
             multiply(1, 0)
             add_bias(0, 0)
             multiply(1, 1)
             add_bias(0, 1)
-            statistics(0)
+            negative_mean(0)
+            centre_and_gain(0, whole)
+            copy_h(2, flipped)
+            copy_last_group()
+            deviation(0)
             for i in range(LAST):
                 if i + 2 < TILES:
                     quantise(i + 2)
-                    if i + 3 < TILES:
-                        prepare(i + 3)
+                if i + 3 < TILES:
+                    copy_h(i + 3, transpose_rows(tiles[i + 3]))
+                    while len(means) < groups_wanted(i + 3):
+                        next_group(mean, "mean")
+                        copy_last_group()
                 if i >= 1:
                     add_h_for_gpsimd(i - 1)
+                    finish_on_gpsimd(i - 1, [whole])
                 spread_h(i)
                 if i + 2 < TILES:
                     multiply(i + 2, 0)
-                if i == 0:
-                    centre_and_gain(i, whole)
-                    add_bias(i + 1, 0)
-                else:
-                    finish_on_gpsimd(i - 1, [whole])
-                    add_bias(i + 1, 0)
+                add_bias(i + 1, 0)
+                if i >= 1:
                     centre_and_gain(i, whole)
                 if i + 2 < TILES:
                     multiply(i + 2, 1)
                 add_bias(i + 1, 1)
-                statistics(i + 1)
-                if i + 4 < TILES and groups_wanted(i + 4) > len(groups_done) + 1:
-                    next_group()
+                negative_mean(i + 1)
+                deviation(i + 1)
+                if i + 4 < TILES and groups_wanted(i + 4) > len(means) + 1:
+                    next_group(mean, "mean")
+                    copy_last_group()
                 scale_and_shift(i, whole)
                 lift_negatives(i, whole)
             back = transpose_back(LAST)

@@ -28,7 +28,7 @@ LEAKY_SLOPE = 0.01
 GROUP = (P // NODES) * NODES
 GROUPS = -(-ROWS // GROUP)
 LAST_WINDOW = ROWS - P
-SHARED = 384
+SHARED = 352
 LAST_STORE = 128
 MEAN_PITCH = 120
 
@@ -124,7 +124,7 @@ def tile_gnnnicheencoder_pa_kernel(
             tiles[0] = windows[0]
             load_window(1)
             for j, vec in enumerate((b_l, ln_g, ln_b)):
-                nc.scalar.dma_start(out=rows[0:1, j, :], in_=vec.unsqueeze(0))
+                nc.sync.dma_start(out=rows[0:1, j, :], in_=vec.unsqueeze(0))
             load_scales()
             load_words(0)
             load_window(2)

@@ -28,7 +28,7 @@ LEAKY_SLOPE = 0.01
 GROUP = (P // NODES) * NODES
 GROUPS = -(-ROWS // GROUP)
 LAST_WINDOW = ROWS - P
-SHARED = 352
+SHARED = 400
 LAST_STORE = 128
 MEAN_PITCH = 120
 

from contextlib import ExitStack

import concourse.mybir as mybir
from concourse.masks import make_identity

F32 = mybir.dt.float32
BF16 = mybir.dt.bfloat16
I32 = mybir.dt.int32
U32 = mybir.dt.uint32
U8 = mybir.dt.uint8
FP8X4 = mybir.dt.float8_e4m3fn_x4
ALU = mybir.AluOpType
ACT = mybir.ActivationFunctionType

P = 128
GRAPHS = 128
NODES = 17
ROWS = GRAPHS * NODES
TILES = ROWS // P
D = 1024
PACK = 4
K_PASS = P * PACK
PASSES = D // K_PASS
N_TILE = 512
HALVES = D // N_TILE
LN_EPS = 1e-5
LEAKY_SLOPE = 0.01
GROUP = (P // NODES) * NODES
GROUPS = -(-ROWS // GROUP)
LAST_WINDOW = ROWS - P
SHARED = 400
LAST_STORE = 128
MEAN_PITCH = 120

FLOPS = 2 * 2 * ROWS * D * D


def tile_gnnnicheencoder_pa_kernel(
    tc, h, W_l_words, W_l_scales, b_l, W_r_words, W_r_scales, ln_g, ln_b, out
):
    nc = tc.nc
    weights = ((W_r_words, W_r_scales), (W_l_words, W_l_scales))
    h_rows = h.rearrange("b n d -> (b n) d")
    out_rows = out.rearrange("b n d -> (b n) d")

    with ExitStack() as stack:
        keep = stack.enter_context(tc.tile_pool(name="keep", bufs=1))
        sides = stack.enter_context(tc.tile_pool(name="sides", bufs=3))
        swap = stack.enter_context(tc.tile_pool(name="swap", bufs=4))
        work = stack.enter_context(tc.tile_pool(name="work", bufs=3))
        small = stack.enter_context(tc.tile_pool(name="small", bufs=4))
        psum_keep = stack.enter_context(tc.psum_pool(name="psum_keep", bufs=1))
        prod = stack.enter_context(tc.psum_pool(name="prod", bufs=3))
        flip = stack.enter_context(tc.psum_pool(name="flip", bufs=1))
        mean = stack.enter_context(tc.psum_pool(name="mean", bufs=1))

        w_planes = keep.tile([P, 2, PASSES, D], U8, align_bytes=64)
        nc.vector.memset(w_planes[:].bitcast(I32), 0)
        rows = keep.tile([P, 3, D], BF16)
        nc.vector.memset(rows[:].bitcast(I32), 0)
        ones = keep.tile([P, P], BF16)
        nc.vector.memset(ones[:], 1.0)
        eps = keep.tile([P, 1], F32)
        nc.vector.memset(eps[:], LN_EPS)
        ident_f32 = keep.tile([P, P], F32)
        make_identity(nc, ident_f32[:])
        ident_bf16 = keep.tile([P, P], BF16)
        nc.vector.tensor_copy(out=ident_bf16[:], in_=ident_f32[:])
        warm = keep.tile([P, 1], F32)
        nc.scalar.activation(out=warm[:], in_=eps[:], func=ACT.Abs_reciprocal_sqrt)

        def make_neighbours(first, columns):
            graphs = columns // NODES
            near = keep.tile([P, columns], BF16, name="near%d" % first)
            nc.gpsimd.memset(near[:], 1.0 / (NODES - 1))
            nc.gpsimd.affine_select(
                out=near[:], in_=near[:], compare_op=ALU.is_ge, fill=0.0,
                base=-first, pattern=[[-NODES, graphs], [0, NODES]], channel_multiplier=1,
            )
            nc.gpsimd.affine_select(
                out=near[:], in_=near[:], compare_op=ALU.is_ge, fill=0.0,
                base=first + NODES - 1, pattern=[[NODES, graphs], [0, NODES]], channel_multiplier=-1,
            )
            nc.gpsimd.affine_select(
                out=near[:], in_=near[:], compare_op=ALU.not_equal, fill=0.0,
                base=-first, pattern=[[-1, columns]], channel_multiplier=1,
            )
            return near

        last_columns = ROWS - (GROUPS - 1) * GROUP
        near_first = make_neighbours(0, GROUP)
        near_last = make_neighbours(P - last_columns, last_columns)

        windows = {}
        tiles = {}

        def load_rows(kind, index, first):
            loaded = keep.tile([P, D], BF16, name="%s%d" % (kind, index))
            nc.sync.dma_start(out=loaded[:], in_=h_rows[first : first + P, :])
            return loaded

        def load_window(a):
            windows[a] = load_rows("window", a, min(a * GROUP, LAST_WINDOW))

        w_words = keep.tile([P, 2, PASSES, D], U32, align_bytes=64)

        def load_scales():
            for w, (words, scales) in enumerate(weights):
                for quad in range(4):
                    nc.sync.dma_start(
                        out=w_planes[32 * quad : 32 * quad + 4, w, :, :].bitcast(I32),
                        in_=scales[:, 4 * quad : 4 * quad + 4, :].rearrange("g r n -> r g n").bitcast(I32),
                    )

        def load_words(w):
            for g in range(PASSES):
                nc.sync.dma_start(
                    out=w_words[:, w, g, :].bitcast(I32),
                    in_=weights[w][0][g].rearrange("p n t -> p (n t)").bitcast(I32),
                )

        def load_all():
            load_window(0)
            tiles[0] = windows[0]
            load_window(1)
            for j, vec in enumerate((b_l, ln_g, ln_b)):
                nc.sync.dma_start(out=rows[0:1, j, :], in_=vec.unsqueeze(0))
            load_scales()
            load_words(0)
            load_window(2)
            load_words(1)
            for i in range(1, TILES):
                tiles[i] = load_rows("tile", i, i * P)
                if i > 1:
                    load_window(i + 1)
            load_window(GROUPS - 1)

        x_ts = {}
        sides_of = {}
        product = {}
        cs, sums_of, neg_means, rstds, centreds, ys, lifts = {}, {}, {}, {}, {}, {}, {}
        halves = [slice(half * N_TILE, (half + 1) * N_TILE) for half in range(HALVES)]
        whole = slice(0, D)
        gpsimd_part = slice(0, D - SHARED)
        vector_part = slice(D - SHARED, D)
        h_sums, y_plus_hs = {}, {}

        def operands_of(j):
            if j not in x_ts:
                x_ts[j] = swap.tile([P, 2, D], BF16, tag="swap", align_bytes=64, name="x_t")
            return x_ts[j]

        def transpose_rows(source):
            pairs = source[:].bitcast(F32)
            flipped = flip.tile([P, PASSES, 2, P], F32)
            for g in range(PASSES):
                for u in range(2):
                    nc.tensor.transpose(
                        out=flipped[:, g, u, :], in_=pairs[:, 256 * g + u : 256 * (g + 1) : 2], identity=ident_f32[:]
                    )
            return flipped

        def copy_h(j, flipped, columns=slice(0, P), first=0):
            nc.scalar.copy(
                out=operands_of(j)[:, 0, :].bitcast(F32).rearrange("p (g b u) -> p g b u", g=PASSES, u=2)[:, :, columns, :],
                in_=flipped[:, :, :, first : first + columns.stop - columns.start].rearrange("p g u b -> p g b u"),
            )

        means = []

        def columns_of(a):
            return min(GROUP, ROWS - a * GROUP)

        def groups_wanted(j):
            return -(-min((j + 1) * P, ROWS) // GROUP)

        def next_group(pool, tag):
            a = len(means)
            near = near_first if a < GROUPS - 1 else near_last
            mean_ps = pool.tile([P, PASSES, PACK, MEAN_PITCH], BF16, tag=tag, name="mean_ps")
            for g in range(PASSES):
                for t in range(PACK):
                    nc.tensor.matmul(
                        out=mean_ps[:, g, t, : columns_of(a)],
                        lhsT=windows[a][:, g * K_PASS + t : (g + 1) * K_PASS : PACK],
                        rhs=near[:],
                        start=True,
                        stop=True,
                    )
            means.append(mean_ps)

        def copy_mean(a, j, copy_out):
            first = max(a * GROUP, j * P)
            end = min(a * GROUP + columns_of(a), (j + 1) * P)
            copy_out(
                out=operands_of(j)[:, 1, :].rearrange("p (g b t) -> p g b t", g=PASSES, t=PACK)[
                    :, :, first - j * P : end - j * P, :
                ],
                in_=means[a][:, :, :, first - a * GROUP : end - a * GROUP].rearrange("p g t b -> p g b t"),
            )

        def copy_last_group():
            a = len(means) - 1
            for j in range(a * GROUP // P, (a * GROUP + columns_of(a) - 1) // P + 1):
                copy_mean(a, j, nc.scalar.copy)

        def quantise(j):
            codes = sides.tile([P, 2 * PASSES * P], U32, align_bytes=64)
            plane = sides.tile([P, 2 * PASSES * P], U8, align_bytes=64)
            nc.vector.quantize_mx(
                out=codes[:].bitcast(FP8X4), scales=plane[:], in_=x_ts[j][:].rearrange("p w d -> p (w d)")
            )
            sides_of[j] = (codes, plane)

        def multiply_part(j, w, half):
            codes, plane = sides_of[j]
            for g in range(PASSES):
                columns = slice((w * PASSES + g) * P, (w * PASSES + g + 1) * P)
                nc.tensor.matmul_mx(
                    out=product[j][half][:],
                    lhsT=codes[:, columns].bitcast(FP8X4),
                    lhsT_scale=plane[:, columns],
                    rhs=w_words[:, w, g, halves[half]].bitcast(FP8X4),
                    rhs_scale=w_planes[:, w, g, halves[half]],
                    start=(w == 0 and g == 0),
                    stop=(w == 1 and g == PASSES - 1),
                )

        def open_product(j):
            product.setdefault(j, []).append(prod.tile([P, N_TILE], F32, tag="prod", name="acc"))

        def multiply(j, half):
            open_product(j)
            for w in range(2):
                multiply_part(j, w, half)

        def spread_over_partitions(j, spread):
            for half in range(HALVES):
                cols = slice(half * N_TILE, (half + 1) * N_TILE)
                nc.tensor.matmul(out=spread[:, cols], lhsT=ones[:], rhs=rows[:, j, cols], start=True, stop=True)

        def add_bias(i, half):
            if half == 0:
                cs[i] = work.tile([P, D], F32, name="c")
                sums_of[i] = small.tile([P, HALVES], F32, name="sums")
            nc.vector.scalar_tensor_tensor(
                out=cs[i][:, halves[half]],
                in0=product[i][half][:],
                scalar=1.0,
                in1=bias_sb[:, halves[half]],
                op0=ALU.mult,
                op1=ALU.add,
                accum_out=sums_of[i][:, half : half + 1],
            )

        def negative_mean(i):
            neg_means[i] = small.tile([P, 1], F32, name="neg_mean")
            scaled_sums = small.tile([P, HALVES], F32)
            nc.scalar.activation(
                out=scaled_sums[:], in_=sums_of[i][:], func=ACT.Copy, scale=-1.0 / D, accum_out=neg_means[i][:]
            )

        def deviation(i):
            squares = work.tile([P, D], BF16)
            sum_sq = small.tile([P, 1], F32)
            nc.scalar.activation(
                out=squares[:], in_=cs[i][:], func=ACT.Square, bias=neg_means[i][:], scale=1.0, accum_out=sum_sq[:]
            )
            rstds[i] = small.tile([P, 1], F32, name="rstd")
            nc.scalar.activation(
                out=rstds[i][:], in_=sum_sq[:], func=ACT.Abs_reciprocal_sqrt, bias=eps[:], scale=1.0 / D
            )

        def centre_and_gain(i, cols):
            if cols.start == 0:
                centreds[i] = work.tile([P, D], F32, name="centred")
            nc.vector.scalar_tensor_tensor(
                out=centreds[i][:, cols], in0=cs[i][:, cols], scalar=neg_means[i][:], in1=gain_ps[:, cols],
                op0=ALU.add, op1=ALU.mult,
            )

        def scale_and_shift(i, cols):
            if cols.start == 0:
                ys[i] = work.tile([P, D], F32, name="y")
            nc.vector.scalar_tensor_tensor(
                out=ys[i][:, cols], in0=centreds[i][:, cols], scalar=rstds[i][:], in1=shift_ps[:, cols],
                op0=ALU.mult, op1=ALU.add,
            )

        def lift_negatives(i, cols):
            if cols.start == 0:
                lifts[i] = work.tile([P, D], F32, name="lift")
            nc.scalar.activation(
                out=lifts[i][:, cols], in_=ys[i][:, cols], func=ACT.Relu, scale=-(1.0 - LEAKY_SLOPE)
            )

        def store(i, cols, result):
            nc.sync.dma_start(out=out_rows[i * P : (i + 1) * P, cols], in_=result)

        def spread_h(i):
            h_sums[i] = psum_keep.tile([P, SHARED], F32, name="h_ps")
            nc.tensor.matmul(out=h_sums[i][:], lhsT=ident_bf16[:], rhs=tiles[i][:, vector_part], start=True, stop=True)

        def add_h_for_gpsimd(i):
            y_plus_hs[i] = work.tile([P, D], F32, name="y_plus_h")
            nc.vector.tensor_tensor(
                out=y_plus_hs[i][:, vector_part], in0=ys[i][:, vector_part], in1=h_sums[i][:], op=ALU.add
            )

        def finish_on_gpsimd(i, parts):
            y_plus_h = y_plus_hs[i]
            nc.gpsimd.tensor_tensor(
                out=y_plus_h[:, gpsimd_part], in0=ys[i][:, gpsimd_part], in1=tiles[i][:, gpsimd_part], op=ALU.add
            )
            result = work.tile([P, D], F32)
            for cols in parts:
                nc.gpsimd.tensor_tensor(out=result[:, cols], in0=y_plus_h[:, cols], in1=lifts[i][:, cols], op=ALU.add)
                store(i, cols, result[:, cols])

        def transpose_back(i):
            back = mean.tile([P, PASSES, PACK, P], BF16, tag="mean", name="back")
            for g in range(PASSES):
                for t in range(PACK):
                    nc.tensor.transpose(
                        out=back[:, g, t, :],
                        in_=x_ts[i][:, 0, g * K_PASS + t : (g + 1) * K_PASS : PACK],
                        identity=ident_bf16[:],
                    )
            return back

        def finish_on_vector(i):
            y_plus_h = work.tile([P, D], F32, name="y_plus_h")
            for g, cols in enumerate(halves):
                nc.vector.tensor_tensor(
                    out=y_plus_h[:, cols].rearrange("r (p t) -> r p t", t=PACK),
                    in0=ys[i][:, cols].rearrange("r (p t) -> r p t", t=PACK),
                    in1=back[:, g].rearrange("r t p -> r p t"),
                    op=ALU.add,
                )
            result_v = work.tile([P, D], F32, name="result")
            for cols in (halves[0], slice(N_TILE, D - LAST_STORE), slice(D - LAST_STORE, D)):
                nc.vector.tensor_tensor(
                    out=result_v[:, cols], in0=y_plus_h[:, cols], in1=lifts[i][:, cols], op=ALU.add
                )
                store(i, cols, result_v[:, cols])

        LAST = TILES - 1

        ordered = {
            mybir.EngineType.DVE, mybir.EngineType.PE, mybir.EngineType.Activation, mybir.EngineType.SP
        }
        with tc.manual_schedule(engines=ordered):
            load_all()
            on_vector, on_scalar = nc.vector.tensor_copy, nc.scalar.copy
            copy_h(0, transpose_rows(windows[0]))
            next_group(mean, "mean")
            copy_mean(0, 0, on_vector)
            next_group(prod, "prod")
            copy_mean(1, 0, on_vector)
            copy_mean(1, 1, on_vector)
            quantise(0)
            copy_h(1, transpose_rows(windows[1]), slice(0, GROUP), P - GROUP)
            bias_ps = prod.tile([P, D], BF16, tag="prod")
            spread_over_partitions(0, bias_ps)
            bias_sb = keep.tile([P, D], BF16)
            nc.scalar.copy(out=bias_sb[:], in_=bias_ps[:])
            gain_ps = psum_keep.tile([P, D], BF16)
            spread_over_partitions(1, gain_ps)
            shift_ps = psum_keep.tile([P, D], BF16)
            spread_over_partitions(2, shift_ps)
            for half in range(HALVES):
                open_product(0)
                multiply_part(0, 0, half)
            copy_h(1, transpose_rows(windows[2]), slice(GROUP, P), P - GROUP)
            next_group(mean, "mean")
            copy_last_group()
            for half in range(HALVES):
                multiply_part(0, 1, half)
            quantise(1)
            flipped = transpose_rows(tiles[2])
            next_group(mean, "mean")
            multiply(1, 0)
            add_bias(0, 0)
            multiply(1, 1)
            add_bias(0, 1)
            negative_mean(0)
            centre_and_gain(0, whole)
            copy_h(2, flipped)
            copy_last_group()
            deviation(0)
            for i in range(LAST):
                if i + 2 < TILES:
                    quantise(i + 2)
                if i + 3 < TILES:
                    copy_h(i + 3, transpose_rows(tiles[i + 3]))
                    while len(means) < groups_wanted(i + 3):
                        next_group(mean, "mean")
                        copy_last_group()
                if i >= 1:
                    add_h_for_gpsimd(i - 1)
                    finish_on_gpsimd(i - 1, [whole])
                spread_h(i)
                if i + 2 < TILES:
                    multiply(i + 2, 0)
                add_bias(i + 1, 0)
                if i >= 1:
                    centre_and_gain(i, whole)
                if i + 2 < TILES:
                    multiply(i + 2, 1)
                add_bias(i + 1, 1)
                negative_mean(i + 1)
                deviation(i + 1)
                if i + 4 < TILES and groups_wanted(i + 4) > len(means) + 1:
                    next_group(mean, "mean")
                    copy_last_group()
                scale_and_shift(i, whole)
                lift_negatives(i, whole)
            back = transpose_back(LAST)
            add_h_for_gpsimd(LAST - 1)
            finish_on_gpsimd(LAST - 1, halves)
            for cols in halves:
                centre_and_gain(LAST, cols)
            for cols in halves:
                scale_and_shift(LAST, cols)
                lift_negatives(LAST, cols)
            finish_on_vector(LAST)
